import numpy as np
import ml_dtypes


def mxq(x, axis, fmt="e4m3"):
    dtype, down = {"e4m3": (ml_dtypes.float8_e4m3fn, 7), "e5m2": (ml_dtypes.float8_e5m2, 14)}[fmt]
    v = np.moveaxis(np.asarray(x, np.float32).astype(ml_dtypes.bfloat16).astype(np.float64), axis, -1)
    blocks = v.reshape(v.shape[:-1] + (-1, 32))
    amax = np.abs(blocks).max(-1, keepdims=True)
    byte = np.maximum(np.where(amax > 0, np.frexp(amax)[1] - 1 + 127, 0) - down, 1)
    scale = np.exp2(byte - 127.0)
    codes = (blocks / scale).astype(np.float32).astype(dtype).astype(np.float64)
    return np.moveaxis((codes * scale).reshape(v.shape), -1, axis)


WIDE = False


def mx_kscale(k):
    if not WIDE:
        return np.ones(k)
    levels = np.array([10, -10, 5, -5, 0])
    a = np.random.permutation(np.resize(levels, k // 512 * 4)).reshape(k // 512, 4)
    idx = np.arange(k)
    return np.exp2(a[idx // 512, idx % 128 // 32])


BF16 = ml_dtypes.bfloat16


def bf(x):
    return np.asarray(x, np.float32).astype(BF16)


def f64(x):
    return np.asarray(x).astype(np.float64)


E2M1 = np.array([0.0, 0.5, 1.0, 1.5, 2.0, 3.0, 4.0, 6.0, -0.0, -0.5, -1.0, -1.5, -2.0, -3.0, -4.0, -6.0])


def pack_weight(w, fmt):
    k, n = w.shape
    w = f64(bf(w)).reshape(k // 32, 32, n)
    amax = np.abs(w).max(1)
    if fmt == "e4m3":
        byte = np.frexp(amax)[1] - 1 + 127 - 7
    else:
        mant, ex = np.frexp(amax / 6.0)
        byte = np.where(mant > 0.5, ex, ex - 1) + 127
    byte = np.clip(np.where(amax > 0, byte, 1), 1, 254)
    scaled = (w * np.exp2(127.0 - byte)[:, None, :]).reshape(k, n).astype(np.float32)
    by_word = np.ascontiguousarray(scaled.reshape(k // 512, 128, 4, n).transpose(0, 1, 3, 2))
    if fmt == "e4m3":
        words = by_word.astype(ml_dtypes.float8_e4m3fn).view(np.uint8)
    else:
        c = by_word.astype(ml_dtypes.float4_e2m1fn).view(np.uint8) & 0xF
        words = c[..., 0::2] | (c[..., 1::2] << 4)
    return np.ascontiguousarray(words), np.ascontiguousarray(byte.astype(np.uint8).reshape(k // 512, 16, n))


def unpack_weight(words, scales, fmt):
    g, p, n, _ = words.shape
    if fmt == "e4m3":
        vals = np.ascontiguousarray(words).view(ml_dtypes.float8_e4m3fn).astype(np.float64)
    else:
        nib = np.empty((g, p, n, 4), np.uint8)
        nib[..., 0::2] = words & 0xF
        nib[..., 1::2] = words >> 4
        vals = E2M1[nib]
    vals = vals * np.repeat(np.exp2(scales.astype(np.float64) - 127.0), 8, axis=1)[..., None]
    return vals.transpose(0, 1, 3, 2).reshape(g * 512, n)


M, N, H = 512, 1024, 2048
RMIN, RMAX = 0.4, 0.99
FMT = "e4m3"


def half_glorot(rows, cols):
    limit = np.sqrt(1.5 / ((rows + cols) / 2.0))
    return np.random.uniform(-limit, limit, (rows, cols))


def setup_inputs():
    s, t = mx_kscale(N), mx_kscale(H)
    inputs = np.random.standard_normal((M, N))
    state_re = np.random.standard_normal((M, H))
    state_im = np.random.standard_normal((M, H))
    C_re = half_glorot(H, N)
    C_im = half_glorot(H, N)
    B_re = half_glorot(N, H)
    B_im = half_glorot(N, H)
    D = np.random.standard_normal(N)
    nu = np.random.uniform(np.log(-np.log(RMAX)), np.log(-np.log(RMIN)), H)
    theta = np.random.uniform(0.0, 3.14 / 10, H)
    gamma = np.sqrt(1.0 - np.exp(-2.0 * np.exp(nu)))
    B_re_words, B_re_scales = pack_weight(B_re / s[:, None], FMT)
    B_im_words, B_im_scales = pack_weight(B_im / s[:, None], FMT)
    C_re_words, C_re_scales = pack_weight(C_re / t[:, None], FMT)
    C_im_words, C_im_scales = pack_weight(C_im / t[:, None], FMT)
    return {"inputs": bf(inputs * s), "state_re": bf(state_re * t), "state_im": bf(state_im * t),
            "B_re_words": B_re_words, "B_re_scales": B_re_scales,
            "B_im_words": B_im_words, "B_im_scales": B_im_scales,
            "C_re_words": C_re_words, "C_re_scales": C_re_scales,
            "C_im_words": C_im_words, "C_im_scales": C_im_scales,
            "D": bf(D / s), "nu": bf(nu), "theta": bf(theta), "gamma": bf(gamma * t)}


def reference(inputs, state_re, state_im, B_re_words, B_re_scales, B_im_words, B_im_scales,
              C_re_words, C_re_scales, C_im_words, C_im_scales, D, nu, theta, gamma):
    u = f64(inputs)
    mag = np.exp(-np.exp(f64(nu)))
    lam_re = mag * np.cos(f64(theta))
    lam_im = mag * np.sin(f64(theta))
    uq = mxq(u, 1, "e4m3")
    new_u_re = f64(gamma) * (uq @ unpack_weight(B_re_words, B_re_scales, FMT))
    new_u_im = f64(gamma) * (uq @ unpack_weight(B_im_words, B_im_scales, FMT))
    x_re = f64(state_re) * lam_re - f64(state_im) * lam_im + new_u_re
    x_im = f64(state_re) * lam_im + f64(state_im) * lam_re + new_u_im
    y = (mxq(x_re, 1, "e4m3") @ unpack_weight(C_re_words, C_re_scales, FMT)) - (mxq(x_im, 1, "e4m3") @ unpack_weight(C_im_words, C_im_scales, FMT)) + f64(D) * u
    return y, x_re, x_im

@@ -1,0 +1,382 @@
+import math
+from contextlib import ExitStack
+
+import concourse.mybir as mybir
+from concourse.masks import make_identity
+
+F32 = mybir.dt.float32
+BF16 = mybir.dt.bfloat16
+I32 = mybir.dt.int32
+U32 = mybir.dt.uint32
+U8 = mybir.dt.uint8
+FP8X4 = mybir.dt.float8_e4m3fn_x4
+ALU = mybir.AluOpType
+ACT = mybir.ActivationFunctionType
+
+P = 128
+ROWS, N_IN, H = 512, 1024, 2048
+K_PASS = 4 * P
+WIDE = 512
+ROW_TILES = ROWS // P
+H_TILES = H // P
+IN_PASSES = N_IN // K_PASS
+H_GROUPS = H // K_PASS
+TILES_PER_GROUP = K_PASS // P
+EARLY_GROUPS = 3
+PARTS = ("re", "im")
+
+FLOPS = 2 * 2 * ROWS * N_IN * H + 2 * 2 * ROWS * H * N_IN
+
+ROUND_MAGIC = 12582912.0
+TWO_PI_HIGH = 6.28125
+TWO_PI_LOW = 2.0 * math.pi - TWO_PI_HIGH
+PI_INSIDE = 3.1415925
+
+
+def tile_linearrecurrentunitcell_kernel(
+    tc,
+    inputs,
+    state_re,
+    state_im,
+    B_re_words,
+    B_re_scales,
+    B_im_words,
+    B_im_scales,
+    C_re_words,
+    C_re_scales,
+    C_im_words,
+    C_im_scales,
+    D,
+    nu,
+    theta,
+    gamma,
+    out_0,
+    out_1,
+    out_2,
+):
+    nc = tc.nc
+    state_in = (state_re, state_im)
+    b_words_in = (B_re_words, B_im_words)
+    b_scales_in = (B_re_scales, B_im_scales)
+    c_words_in = (C_re_words, C_im_words)
+    c_scales_in = (C_re_scales, C_im_scales)
+    new_out = (out_1, out_2)
+
+    with ExitStack() as ctx:
+        keep = ctx.enter_context(tc.tile_pool(name="keep", bufs=1))
+        acc_pool = ctx.enter_context(tc.tile_pool(name="acc", bufs=3))
+        group_pool = ctx.enter_context(tc.tile_pool(name="group", bufs=2))
+        quant_pool = ctx.enter_context(tc.tile_pool(name="quant", bufs=3))
+        bank = ctx.enter_context(tc.psum_pool(name="bank", bufs=1))
+        word_bank = ctx.enter_context(tc.psum_pool(name="word_bank", bufs=2))
+        ctx.enter_context(tc.manual_schedule())
+
+        vec_rows = keep.tile([P, P], BF16)
+        nc.vector.memset(vec_rows[:], 0.0)
+        for v, vec in enumerate((nu, theta, gamma)):
+            nc.sync.dma_start(
+                out=vec_rows[v * H_TILES : (v + 1) * H_TILES, :],
+                in_=vec.rearrange("(r j) -> r j", j=P),
+            )
+
+        u_sb = keep.tile([P, ROW_TILES, N_IN], BF16)
+        for mi in range(ROW_TILES):
+            nc.sync.dma_start(out=u_sb[:, mi, :], in_=inputs[mi * P : (mi + 1) * P, :])
+
+        b_planes = keep.tile([P, H], U8, align_bytes=64)
+        nc.vector.memset(b_planes[:].bitcast(I32), 0)
+        c_planes = keep.tile([P, 2, N_IN], U8, align_bytes=64)
+        nc.vector.memset(c_planes[:].bitcast(I32), 0)
+        for c in range(2):
+            for quad in range(4):
+                first = 32 * quad + 8 * c
+                nc.sync.dma_start(
+                    out=b_planes[first : first + 8, :].bitcast(I32),
+                    in_=b_scales_in[c][:, 4 * quad : 4 * quad + 4, :].bitcast(I32),
+                )
+
+        b_words = keep.tile([P, 2, IN_PASSES, H], U32, align_bytes=64)
+        state_sb = [
+            keep.tile([P, ROW_TILES, H], BF16, name="state_%s" % part) for part in PARTS
+        ]
+        for g in range(H_GROUPS):
+            cols = slice(g * K_PASS, (g + 1) * K_PASS)
+            for c in range(2):
+                nc.sync.dma_start(
+                    out=state_sb[c][:, :, cols],
+                    in_=state_in[c].rearrange("(mi p) h -> p mi h", p=P)[:, :, cols],
+                )
+            for c in range(2):
+                for kp in range(IN_PASSES):
+                    nc.sync.dma_start(
+                        out=b_words[:, c, kp, cols].bitcast(I32),
+                        in_=b_words_in[c][kp]
+                        .rearrange("p n t -> p (n t)")[:, 4 * g * K_PASS : 4 * (g + 1) * K_PASS]
+                        .bitcast(I32),
+                    )
+
+        for c in range(2):
+            for quad in range(4):
+                nc.sync.dma_start(
+                    out=c_planes[32 * quad : 32 * quad + 16, c, :].bitcast(I32),
+                    in_=c_scales_in[c][:, 4 * quad : 4 * quad + 4, :].bitcast(I32),
+                )
+        c_words = keep.tile([P, 2, H_GROUPS, N_IN], U32, align_bytes=64)
+        for g in range(H_GROUPS):
+            for c in range(2):
+                nc.sync.dma_start(
+                    out=c_words[:, c, g, :].bitcast(I32),
+                    in_=c_words_in[c][g].rearrange("p n t -> p (n t)").bitcast(I32),
+                )
+        d_all = keep.tile([P, N_IN], BF16)
+        nc.sync.dma_start(out=d_all[:], in_=D.partition_broadcast(P))
+
+        ident_bf16 = keep.tile([P, P], BF16)
+        make_identity(nc, ident_bf16[:])
+        ident_f32 = keep.tile([P, P], F32)
+        make_identity(nc, ident_f32[:])
+
+        def lay_side_by_side(engine_copy, grouped, words_ps, rows_half):
+            engine_copy(
+                out=grouped[:]
+                .bitcast(F32)
+                .rearrange("p (m half) -> p m half", half=2)[
+                    :, rows_half * 2 * P : (rows_half + 1) * 2 * P, :
+                ],
+                in_=words_ps[:].rearrange("p half m -> p m half"),
+            )
+
+        def transpose_words(source, first_word, rows_half):
+            words_ps = word_bank.tile([P, 2, 2 * P], F32, name="words_ps")
+            for half in range(2):
+                for ml in range(2):
+                    nc.tensor.transpose(
+                        words_ps[:, half, ml * P : (ml + 1) * P],
+                        source[:, 2 * rows_half + ml, :].bitcast(F32)[
+                            :, first_word + half : first_word + 2 * P : 2
+                        ],
+                        ident_f32[:],
+                    )
+            return words_ps
+
+        vec_ps = bank.tile([P, P], BF16, tag="state_t_re", name="vec_ps")
+        nc.tensor.transpose(vec_ps[:], vec_rows[:], ident_bf16[:])
+        vec_cols = keep.tile([P, 3 * H_TILES], F32)
+        nc.vector.tensor_copy(out=vec_cols[:], in_=vec_ps[:, 0 : 3 * H_TILES])
+        nu_cols = vec_cols[:, 0:H_TILES]
+        theta_cols = vec_cols[:, H_TILES : 2 * H_TILES]
+        gamma_cols = vec_cols[:, 2 * H_TILES : 3 * H_TILES]
+
+        decay = keep.tile([P, H_TILES], F32)
+        nc.scalar.activation(out=decay[:], in_=nu_cols, func=ACT.Exp)
+        nc.scalar.activation(out=decay[:], in_=decay[:], func=ACT.Exp, scale=-1.0)
+
+        angle = keep.tile([P, 2 * H_TILES], F32)
+        nc.vector.tensor_copy(out=angle[:, 0:H_TILES], in_=theta_cols)
+        nc.vector.tensor_scalar_add(out=angle[:, H_TILES : 2 * H_TILES], in0=theta_cols, scalar1=0.5 * math.pi)
+        turns = keep.tile([P, 2 * H_TILES], F32)
+        nc.vector.tensor_scalar(
+            out=turns[:], in0=angle[:], scalar1=0.5 / math.pi, scalar2=ROUND_MAGIC, op0=ALU.mult, op1=ALU.add
+        )
+        nc.vector.tensor_scalar_add(out=turns[:], in0=turns[:], scalar1=-ROUND_MAGIC)
+        nc.vector.scalar_tensor_tensor(
+            out=angle[:], in0=turns[:], scalar=-TWO_PI_HIGH, in1=angle[:], op0=ALU.mult, op1=ALU.add
+        )
+        nc.vector.scalar_tensor_tensor(
+            out=angle[:], in0=turns[:], scalar=-TWO_PI_LOW, in1=angle[:], op0=ALU.mult, op1=ALU.add
+        )
+        nc.vector.tensor_scalar(
+            out=angle[:], in0=angle[:], scalar1=PI_INSIDE, scalar2=-PI_INSIDE, op0=ALU.min, op1=ALU.max
+        )
+        sin_cos = keep.tile([P, 2 * H_TILES], F32)
+        nc.scalar.activation(out=sin_cos[:], in_=angle[:], func=ACT.Sin)
+
+        u_words = keep.tile([P, IN_PASSES, ROWS], U32, align_bytes=64)
+        u_planes = keep.tile([P, IN_PASSES, ROWS], U8, align_bytes=64)
+        for kp in range(IN_PASSES):
+            u_grouped = quant_pool.tile([P, 4 * ROWS], BF16, align_bytes=64, name="grouped")
+            for rows_half in range(2):
+                words_ps = transpose_words(u_sb, kp * 2 * P, rows_half)
+                copy = nc.scalar.copy if rows_half == 0 else nc.vector.tensor_copy
+                lay_side_by_side(copy, u_grouped, words_ps, rows_half)
+            nc.vector.quantize_mx(
+                out=u_words[:, kp, :].bitcast(FP8X4), scales=u_planes[:, kp, :], in_=u_grouped[:]
+            )
+
+        lam_re = keep.tile([P, H_TILES], F32)
+        nc.vector.tensor_mul(out=lam_re[:], in0=decay[:], in1=sin_cos[:, H_TILES : 2 * H_TILES])
+        lam_im = keep.tile([P, H_TILES], F32)
+        nc.vector.tensor_mul(out=lam_im[:], in0=decay[:], in1=sin_cos[:, 0:H_TILES])
+        neg_lam_im = keep.tile([P, H_TILES], F32)
+        nc.vector.tensor_scalar_mul(out=neg_lam_im[:], in0=lam_im[:], scalar1=-1.0)
+
+        state_t = {}
+        product = {}
+        new_t = {}
+        new_ps = {}
+        new_rows = {}
+        new_bf16 = {}
+        new_grouped = {}
+        word_tiles = {}
+
+        x_words = keep.tile([P, 2, H_GROUPS, ROWS], U32, align_bytes=64)
+        x_planes = keep.tile([P, 2, H_GROUPS, ROWS], U8, align_bytes=64)
+        y_sum = keep.tile([P, ROW_TILES, N_IN], F32)
+
+        def transpose_state(i):
+            for c in range(2):
+                t = bank.tile([P, ROWS], BF16, tag="state_t_%s" % PARTS[c], name="state_t_%s" % PARTS[c])
+                for mi in range(ROW_TILES):
+                    nc.tensor.transpose(
+                        t[:, mi * P : (mi + 1) * P],
+                        state_sb[c][:, mi, i * P : (i + 1) * P],
+                        ident_bf16[:],
+                    )
+                state_t[(i, c)] = t
+
+        def rotate_on_scalar(i):
+            one = slice(i, i + 1)
+            for c, lam in enumerate((lam_re, lam_im)):
+                t = acc_pool.tile([P, ROWS], F32, name="new_t_%s" % PARTS[c])
+                nc.scalar.activation(out=t[:], in_=state_t[(i, 0)][:], func=ACT.Copy, scale=lam[:, one])
+                new_t[(i, c)] = t
+
+        def rotate_on_vector(i):
+            one = slice(i, i + 1)
+            for c, lam in enumerate((neg_lam_im, lam_re)):
+                nc.vector.scalar_tensor_tensor(
+                    out=new_t[(i, c)][:],
+                    in0=state_t[(i, 1)][:],
+                    scalar=lam[:, one],
+                    in1=new_t[(i, c)][:],
+                    op0=ALU.mult,
+                    op1=ALU.add,
+                )
+
+        def multiply_by_b(i):
+            cols = slice(i * P, (i + 1) * P)
+            for c in range(2):
+                acc = bank.tile([P, ROWS], F32, tag="product_%s" % PARTS[c], name="product_%s" % PARTS[c])
+                for kp in range(IN_PASSES):
+                    nc.tensor.matmul_mx(
+                        out=acc[:],
+                        lhsT=b_words[:, c, kp, cols].bitcast(FP8X4),
+                        lhsT_scale=b_planes[8 * c + 4 * kp : P, cols],
+                        rhs=u_words[:, kp, :].bitcast(FP8X4),
+                        rhs_scale=u_planes[:, kp, :],
+                        start=(kp == 0),
+                        stop=(kp == IN_PASSES - 1),
+                    )
+                product[(i, c)] = acc
+
+        def add_product(i):
+            for c in range(2):
+                nc.vector.scalar_tensor_tensor(
+                    out=new_t[(i, c)][:],
+                    in0=product[(i, c)][:],
+                    scalar=gamma_cols[:, i : i + 1],
+                    in1=new_t[(i, c)][:],
+                    op0=ALU.mult,
+                    op1=ALU.add,
+                )
+
+        def transpose_back(i):
+            for c in range(2):
+                t = bank.tile([P, ROW_TILES, P], F32, tag="new_ps_%s" % PARTS[c], name="new_ps_%s" % PARTS[c])
+                for mi in range(ROW_TILES):
+                    nc.tensor.transpose(t[:, mi, :], new_t[(i, c)][:, mi * P : (mi + 1) * P], ident_f32[:])
+                new_ps[(i, c)] = t
+
+        def take_out(i):
+            g, a = divmod(i, TILES_PER_GROUP)
+            cols = slice(a * P, (a + 1) * P)
+            for c in range(2):
+                if a == 0:
+                    new_rows[(g, c)] = group_pool.tile([P, ROW_TILES, K_PASS], F32, name="new_rows_%s" % PARTS[c])
+                    new_bf16[(g, c)] = group_pool.tile([P, ROW_TILES, K_PASS], BF16, name="new_bf16_%s" % PARTS[c])
+                nc.scalar.copy(out=new_rows[(g, c)][:, :, cols], in_=new_ps[(i, c)][:])
+                nc.gpsimd.tensor_scalar(
+                    out=new_bf16[(g, c)][:, :, cols],
+                    in0=new_rows[(g, c)][:, :, cols],
+                    scalar1=(1.0 if c == 0 else -1.0),
+                    scalar2=0.0,
+                    op0=ALU.mult,
+                    op1=ALU.add,
+                )
+                if a == TILES_PER_GROUP - 1:
+                    nc.sync.dma_start(
+                        out=new_out[c].rearrange("(mi p) h -> p mi h", p=P)[:, :, g * K_PASS : (g + 1) * K_PASS],
+                        in_=new_rows[(g, c)][:],
+                    )
+
+        def transpose_quarter(j):
+            g, rest = divmod(j, 4)
+            c, rows_half = divmod(rest, 2)
+            word_tiles[j] = transpose_words(new_bf16[(g, c)], 0, rows_half)
+
+        def copy_quarter(j):
+            g, rest = divmod(j, 4)
+            c, rows_half = divmod(rest, 2)
+            if rows_half == 0:
+                new_grouped[(g, c)] = quant_pool.tile([P, 4 * ROWS], BF16, align_bytes=64, name="grouped")
+            copy = nc.scalar.copy if rows_half == 0 else nc.vector.tensor_copy
+            lay_side_by_side(copy, new_grouped[(g, c)], word_tiles[j], rows_half)
+
+        def quantise_new(pair):
+            g, c = divmod(pair, 2)
+            nc.vector.quantize_mx(
+                out=x_words[:, c, g, :].bitcast(FP8X4), scales=x_planes[:, c, g, :], in_=new_grouped[(g, c)][:]
+            )
+
+        def add_to_y(mi, groups):
+            rows = slice(mi * P, (mi + 1) * P)
+            passes = [(g, c) for g in groups for c in range(2)]
+            for n in range(N_IN // WIDE):
+                cols = slice(n * WIDE, (n + 1) * WIDE)
+                acc = bank.tile([P, WIDE], F32, tag="product_%s" % PARTS[n], name="y_ps_%d" % n)
+                for index, (g, c) in enumerate(passes):
+                    nc.tensor.matmul_mx(
+                        out=acc[:],
+                        lhsT=x_words[:, c, g, rows].bitcast(FP8X4),
+                        lhsT_scale=x_planes[:, c, g, rows],
+                        rhs=c_words[:, c, g, cols].bitcast(FP8X4),
+                        rhs_scale=c_planes[4 * g : P, c, cols],
+                        start=(index == 0),
+                        stop=(index == len(passes) - 1),
+                    )
+                nc.vector.tensor_add(out=y_sum[:, mi, cols], in0=acc[:], in1=y_sum[:, mi, cols])
+
+        QUARTERS = 4 * H_GROUPS
+        QUARTER_LAG = TILES_PER_GROUP
+        QUANTISE_LAG = QUARTER_LAG + 2
+        transpose_state(0)
+        rotate_on_scalar(0)
+        rotate_on_vector(0)
+        multiply_by_b(0)
+        for i in range(H_TILES + QUARTER_LAG + 1):
+            j = i - QUARTER_LAG
+            if i + 1 < H_TILES:
+                transpose_state(i + 1)
+            if 0 <= j < QUARTERS:
+                transpose_quarter(j)
+            if i < H_TILES:
+                add_product(i)
+            if i >= QUANTISE_LAG and (i - QUANTISE_LAG) % 2 == 0:
+                quantise_new((i - QUANTISE_LAG) // 2)
+            if i + 1 < H_TILES:
+                rotate_on_scalar(i + 1)
+                rotate_on_vector(i + 1)
+                multiply_by_b(i + 1)
+            if 0 <= j < QUARTERS:
+                copy_quarter(j)
+            if i < H_TILES:
+                transpose_back(i)
+                take_out(i)
+            if H_TILES <= i < H_TILES + ROW_TILES:
+                mi = i - H_TILES
+                nc.vector.tensor_mul(out=y_sum[:, mi, :], in0=u_sb[:, mi, :], in1=d_all[:])
+                add_to_y(mi, range(EARLY_GROUPS))
+
+        for mi in range(ROW_TILES):
+            add_to_y(mi, range(EARLY_GROUPS, H_GROUPS))
+            nc.sync.dma_start(out=out_0[mi * P : (mi + 1) * P, :], in_=y_sum[:, mi, :])

@@ -22,7 +22,7 @@ H_TILES = H // P
 IN_PASSES = N_IN // K_PASS
 H_GROUPS = H // K_PASS
 TILES_PER_GROUP = K_PASS // P
-EARLY_GROUPS = 3
+EARLY_GROUPS = 2
 PARTS = ("re", "im")
 
 FLOPS = 2 * 2 * ROWS * N_IN * H + 2 * 2 * ROWS * H * N_IN
@@ -68,7 +68,7 @@ def tile_linearrecurrentunitcell_kernel(
         group_pool = ctx.enter_context(tc.tile_pool(name="group", bufs=2))
         quant_pool = ctx.enter_context(tc.tile_pool(name="quant", bufs=3))
         bank = ctx.enter_context(tc.psum_pool(name="bank", bufs=1))
-        word_bank = ctx.enter_context(tc.psum_pool(name="word_bank", bufs=2))
+        sum_bank = ctx.enter_context(tc.psum_pool(name="sum_bank", bufs=3))
         ctx.enter_context(tc.manual_schedule())
 
         vec_rows = keep.tile([P, P], BF16)
@@ -146,8 +146,7 @@ def tile_linearrecurrentunitcell_kernel(
                 in_=words_ps[:].rearrange("p half m -> p m half"),
             )
 
-        def transpose_words(source, first_word, rows_half):
-            words_ps = word_bank.tile([P, 2, 2 * P], F32, name="words_ps")
+        def transpose_words(words_ps, source, first_word, rows_half):
             for half in range(2):
                 for ml in range(2):
                     nc.tensor.transpose(
@@ -157,7 +156,6 @@ def tile_linearrecurrentunitcell_kernel(
                         ],
                         ident_f32[:],
                     )
-            return words_ps
 
         vec_ps = bank.tile([P, P], BF16, tag="state_t_re", name="vec_ps")
         nc.tensor.transpose(vec_ps[:], vec_rows[:], ident_bf16[:])
@@ -196,7 +194,8 @@ def tile_linearrecurrentunitcell_kernel(
         for kp in range(IN_PASSES):
             u_grouped = quant_pool.tile([P, 4 * ROWS], BF16, align_bytes=64, name="grouped")
             for rows_half in range(2):
-                words_ps = transpose_words(u_sb, kp * 2 * P, rows_half)
+                words_ps = sum_bank.tile([P, 2, 2 * P], F32, tag="mx_sum", name="u_words_ps")
+                transpose_words(words_ps, u_sb, kp * 2 * P, rows_half)
                 copy = nc.scalar.copy if rows_half == 0 else nc.vector.tensor_copy
                 lay_side_by_side(copy, u_grouped, words_ps, rows_half)
             nc.vector.quantize_mx(
@@ -223,16 +222,15 @@ def tile_linearrecurrentunitcell_kernel(
         x_planes = keep.tile([P, 2, H_GROUPS, ROWS], U8, align_bytes=64)
         y_sum = keep.tile([P, ROW_TILES, N_IN], F32)
 
-        def transpose_state(i):
-            for c in range(2):
-                t = bank.tile([P, ROWS], BF16, tag="state_t_%s" % PARTS[c], name="state_t_%s" % PARTS[c])
-                for mi in range(ROW_TILES):
-                    nc.tensor.transpose(
-                        t[:, mi * P : (mi + 1) * P],
-                        state_sb[c][:, mi, i * P : (i + 1) * P],
-                        ident_bf16[:],
-                    )
-                state_t[(i, c)] = t
+        def transpose_state(i, c):
+            t = bank.tile([P, ROWS], BF16, tag="state_t_%s" % PARTS[c], name="state_t_%s" % PARTS[c])
+            for mi in range(ROW_TILES):
+                nc.tensor.transpose(
+                    t[:, mi * P : (mi + 1) * P],
+                    state_sb[c][:, mi, i * P : (i + 1) * P],
+                    ident_bf16[:],
+                )
+            state_t[(i, c)] = t
 
         def rotate_on_scalar(i):
             one = slice(i, i + 1)
@@ -256,7 +254,7 @@ def tile_linearrecurrentunitcell_kernel(
         def multiply_by_b(i):
             cols = slice(i * P, (i + 1) * P)
             for c in range(2):
-                acc = bank.tile([P, ROWS], F32, tag="product_%s" % PARTS[c], name="product_%s" % PARTS[c])
+                acc = sum_bank.tile([P, ROWS], F32, tag="mx_sum", name="product_%s" % PARTS[c])
                 for kp in range(IN_PASSES):
                     nc.tensor.matmul_mx(
                         out=acc[:],
@@ -312,15 +310,15 @@ def tile_linearrecurrentunitcell_kernel(
         def transpose_quarter(j):
             g, rest = divmod(j, 4)
             c, rows_half = divmod(rest, 2)
-            word_tiles[j] = transpose_words(new_bf16[(g, c)], 0, rows_half)
+            word_tiles[j] = bank.tile([P, 2, 2 * P], F32, name="new_words_ps")
+            transpose_words(word_tiles[j], new_bf16[(g, c)], 0, rows_half)
 
         def copy_quarter(j):
             g, rest = divmod(j, 4)
             c, rows_half = divmod(rest, 2)
             if rows_half == 0:
                 new_grouped[(g, c)] = quant_pool.tile([P, 4 * ROWS], BF16, align_bytes=64, name="grouped")
-            copy = nc.scalar.copy if rows_half == 0 else nc.vector.tensor_copy
-            lay_side_by_side(copy, new_grouped[(g, c)], word_tiles[j], rows_half)
+            lay_side_by_side(nc.scalar.copy, new_grouped[(g, c)], word_tiles[j], rows_half)
 
         def quantise_new(pair):
             g, c = divmod(pair, 2)
@@ -333,7 +331,7 @@ def tile_linearrecurrentunitcell_kernel(
             passes = [(g, c) for g in groups for c in range(2)]
             for n in range(N_IN // WIDE):
                 cols = slice(n * WIDE, (n + 1) * WIDE)
-                acc = bank.tile([P, WIDE], F32, tag="product_%s" % PARTS[n], name="y_ps_%d" % n)
+                acc = sum_bank.tile([P, WIDE], F32, tag="mx_sum", name="y_ps")
                 for index, (g, c) in enumerate(passes):
                     nc.tensor.matmul_mx(
                         out=acc[:],
@@ -347,28 +345,34 @@ def tile_linearrecurrentunitcell_kernel(
                 nc.vector.tensor_add(out=y_sum[:, mi, cols], in0=acc[:], in1=y_sum[:, mi, cols])
 
         QUARTERS = 4 * H_GROUPS
-        QUARTER_LAG = TILES_PER_GROUP
+        QUARTER_LAG = TILES_PER_GROUP + 1
         QUANTISE_LAG = QUARTER_LAG + 2
-        transpose_state(0)
+        transpose_state(0, 0)
         rotate_on_scalar(0)
+        transpose_state(0, 1)
         rotate_on_vector(0)
+        transpose_state(1, 0)
+        rotate_on_scalar(1)
         multiply_by_b(0)
-        for i in range(H_TILES + QUARTER_LAG + 1):
+        for i in range(QUARTERS + QUANTISE_LAG - 1):
             j = i - QUARTER_LAG
             if i + 1 < H_TILES:
-                transpose_state(i + 1)
+                transpose_state(i + 1, 1)
             if 0 <= j < QUARTERS:
                 transpose_quarter(j)
+            if i + 2 < H_TILES:
+                transpose_state(i + 2, 0)
             if i < H_TILES:
                 add_product(i)
             if i >= QUANTISE_LAG and (i - QUANTISE_LAG) % 2 == 0:
                 quantise_new((i - QUANTISE_LAG) // 2)
-            if i + 1 < H_TILES:
-                rotate_on_scalar(i + 1)
-                rotate_on_vector(i + 1)
-                multiply_by_b(i + 1)
             if 0 <= j < QUARTERS:
                 copy_quarter(j)
+            if i + 2 < H_TILES:
+                rotate_on_scalar(i + 2)
+            if i + 1 < H_TILES:
+                rotate_on_vector(i + 1)
+                multiply_by_b(i + 1)
             if i < H_TILES:
                 transpose_back(i)
                 take_out(i)

@@ -251,21 +251,20 @@ def tile_linearrecurrentunitcell_kernel(
                     op1=ALU.add,
                 )
 
-        def multiply_by_b(i):
+        def multiply_by_b(i, c):
             cols = slice(i * P, (i + 1) * P)
-            for c in range(2):
-                acc = sum_bank.tile([P, ROWS], F32, tag="mx_sum", name="product_%s" % PARTS[c])
-                for kp in range(IN_PASSES):
-                    nc.tensor.matmul_mx(
-                        out=acc[:],
-                        lhsT=b_words[:, c, kp, cols].bitcast(FP8X4),
-                        lhsT_scale=b_planes[8 * c + 4 * kp : P, cols],
-                        rhs=u_words[:, kp, :].bitcast(FP8X4),
-                        rhs_scale=u_planes[:, kp, :],
-                        start=(kp == 0),
-                        stop=(kp == IN_PASSES - 1),
-                    )
-                product[(i, c)] = acc
+            acc = sum_bank.tile([P, ROWS], F32, tag="mx_sum", name="product_%s" % PARTS[c])
+            for kp in range(IN_PASSES):
+                nc.tensor.matmul_mx(
+                    out=acc[:],
+                    lhsT=b_words[:, c, kp, cols].bitcast(FP8X4),
+                    lhsT_scale=b_planes[8 * c + 4 * kp : P, cols],
+                    rhs=u_words[:, kp, :].bitcast(FP8X4),
+                    rhs_scale=u_planes[:, kp, :],
+                    start=(kp == 0),
+                    stop=(kp == IN_PASSES - 1),
+                )
+            product[(i, c)] = acc
 
         def add_product(i):
             for c in range(2):
@@ -353,13 +352,16 @@ def tile_linearrecurrentunitcell_kernel(
         rotate_on_vector(0)
         transpose_state(1, 0)
         rotate_on_scalar(1)
-        multiply_by_b(0)
+        multiply_by_b(0, 0)
+        multiply_by_b(0, 1)
         for i in range(QUARTERS + QUANTISE_LAG - 1):
             j = i - QUARTER_LAG
             if i + 1 < H_TILES:
                 transpose_state(i + 1, 1)
             if 0 <= j < QUARTERS:
                 transpose_quarter(j)
+            if i + 1 < H_TILES:
+                multiply_by_b(i + 1, 0)
             if i + 2 < H_TILES:
                 transpose_state(i + 2, 0)
             if i < H_TILES:
@@ -372,9 +374,11 @@ def tile_linearrecurrentunitcell_kernel(
                 rotate_on_scalar(i + 2)
             if i + 1 < H_TILES:
                 rotate_on_vector(i + 1)
-                multiply_by_b(i + 1)
             if i < H_TILES:
                 transpose_back(i)
+            if i + 1 < H_TILES:
+                multiply_by_b(i + 1, 1)
+            if i < H_TILES:
                 take_out(i)
             if H_TILES <= i < H_TILES + ROW_TILES:
                 mi = i - H_TILES

@@ -80,8 +80,7 @@ def tile_linearrecurrentunitcell_kernel(
             )
 
         u_sb = keep.tile([P, ROW_TILES, N_IN], BF16)
-        for mi in range(ROW_TILES):
-            nc.sync.dma_start(out=u_sb[:, mi, :], in_=inputs[mi * P : (mi + 1) * P, :])
+        nc.sync.dma_start(out=u_sb[:], in_=inputs.rearrange("(mi p) k -> p mi k", p=P))
 
         b_planes = keep.tile([P, H], U8, align_bytes=64)
         nc.vector.memset(b_planes[:].bitcast(I32), 0)
@@ -146,14 +145,12 @@ def tile_linearrecurrentunitcell_kernel(
                 in_=words_ps[:].rearrange("p half m -> p m half"),
             )
 
-        def transpose_words(words_ps, source, first_word, rows_half):
+        def transpose_words(words_ps, words_of, rows_half):
             for half in range(2):
                 for ml in range(2):
                     nc.tensor.transpose(
                         words_ps[:, half, ml * P : (ml + 1) * P],
-                        source[:, 2 * rows_half + ml, :].bitcast(F32)[
-                            :, first_word + half : first_word + 2 * P : 2
-                        ],
+                        words_of(2 * rows_half + ml, half),
                         ident_f32[:],
                     )
 
@@ -195,7 +192,11 @@ def tile_linearrecurrentunitcell_kernel(
             u_grouped = quant_pool.tile([P, 4 * ROWS], BF16, align_bytes=64, name="grouped")
             for rows_half in range(2):
                 words_ps = sum_bank.tile([P, 2, 2 * P], F32, tag="mx_sum", name="u_words_ps")
-                transpose_words(words_ps, u_sb, kp * 2 * P, rows_half)
+                transpose_words(
+                    words_ps,
+                    lambda mi, half: u_sb[:, mi, :].bitcast(F32)[:, 2 * P * kp + half : 2 * P * (kp + 1) : 2],
+                    rows_half,
+                )
                 copy = nc.scalar.copy if rows_half == 0 else nc.vector.tensor_copy
                 lay_side_by_side(copy, u_grouped, words_ps, rows_half)
             nc.vector.quantize_mx(
@@ -225,10 +226,12 @@ def tile_linearrecurrentunitcell_kernel(
         def transpose_state(i, c):
             t = bank.tile([P, ROWS], BF16, tag="state_t_%s" % PARTS[c], name="state_t_%s" % PARTS[c])
             for mi in range(ROW_TILES):
-                nc.tensor.transpose(
-                    t[:, mi * P : (mi + 1) * P],
-                    state_sb[c][:, mi, i * P : (i + 1) * P],
-                    ident_bf16[:],
+                nc.tensor.matmul(
+                    out=t[:, mi * P : (mi + 1) * P],
+                    lhsT=state_sb[c][:, mi, i * P : (i + 1) * P],
+                    rhs=ident_bf16[:],
+                    start=True,
+                    stop=True,
                 )
             state_t[(i, c)] = t
 
@@ -290,16 +293,19 @@ def tile_linearrecurrentunitcell_kernel(
             for c in range(2):
                 if a == 0:
                     new_rows[(g, c)] = group_pool.tile([P, ROW_TILES, K_PASS], F32, name="new_rows_%s" % PARTS[c])
-                    new_bf16[(g, c)] = group_pool.tile([P, ROW_TILES, K_PASS], BF16, name="new_bf16_%s" % PARTS[c])
+                    new_bf16[(g, c)] = group_pool.tile([P, ROW_TILES, 2, P, 2], BF16, name="new_bf16_%s" % PARTS[c])
                 nc.scalar.copy(out=new_rows[(g, c)][:, :, cols], in_=new_ps[(i, c)][:])
-                nc.gpsimd.tensor_scalar(
-                    out=new_bf16[(g, c)][:, :, cols],
-                    in0=new_rows[(g, c)][:, :, cols],
-                    scalar1=(1.0 if c == 0 else -1.0),
-                    scalar2=0.0,
-                    op0=ALU.mult,
-                    op1=ALU.add,
-                )
+                for half in range(2):
+                    nc.gpsimd.tensor_scalar(
+                        out=new_bf16[(g, c)][:, :, half, a * (P // 4) : (a + 1) * (P // 4), :],
+                        in0=new_rows[(g, c)][:, :, cols].rearrange(
+                            "p mi (q half e) -> p mi half q e", half=2, e=2
+                        )[:, :, half],
+                        scalar1=(1.0 if c == 0 else -1.0),
+                        scalar2=0.0,
+                        op0=ALU.mult,
+                        op1=ALU.add,
+                    )
                 if a == TILES_PER_GROUP - 1:
                     nc.sync.dma_start(
                         out=new_out[c].rearrange("(mi p) h -> p mi h", p=P)[:, :, g * K_PASS : (g + 1) * K_PASS],
@@ -310,7 +316,11 @@ def tile_linearrecurrentunitcell_kernel(
             g, rest = divmod(j, 4)
             c, rows_half = divmod(rest, 2)
             word_tiles[j] = bank.tile([P, 2, 2 * P], F32, name="new_words_ps")
-            transpose_words(word_tiles[j], new_bf16[(g, c)], 0, rows_half)
+            transpose_words(
+                word_tiles[j],
+                lambda mi, half: new_bf16[(g, c)][:, mi, half].rearrange("p q e -> p (q e)").bitcast(F32),
+                rows_half,
+            )
 
         def copy_quarter(j):
             g, rest = divmod(j, 4)
@@ -342,6 +352,8 @@ def tile_linearrecurrentunitcell_kernel(
                         stop=(index == len(passes) - 1),
                     )
                 nc.vector.tensor_add(out=y_sum[:, mi, cols], in0=acc[:], in1=y_sum[:, mi, cols])
+                if H_GROUPS - 1 in groups:
+                    nc.sync.dma_start(out=out_0[rows, cols], in_=y_sum[:, mi, cols])
 
         QUARTERS = 4 * H_GROUPS
         QUARTER_LAG = TILES_PER_GROUP + 1
@@ -358,27 +370,25 @@ def tile_linearrecurrentunitcell_kernel(
             j = i - QUARTER_LAG
             if i + 1 < H_TILES:
                 transpose_state(i + 1, 1)
-            if 0 <= j < QUARTERS:
-                transpose_quarter(j)
-            if i + 1 < H_TILES:
                 multiply_by_b(i + 1, 0)
             if i + 2 < H_TILES:
                 transpose_state(i + 2, 0)
             if i < H_TILES:
                 add_product(i)
+            if i + 1 < H_TILES:
+                multiply_by_b(i + 1, 1)
+            if 0 <= j < QUARTERS:
+                transpose_quarter(j)
             if i >= QUANTISE_LAG and (i - QUANTISE_LAG) % 2 == 0:
                 quantise_new((i - QUANTISE_LAG) // 2)
-            if 0 <= j < QUARTERS:
-                copy_quarter(j)
             if i + 2 < H_TILES:
                 rotate_on_scalar(i + 2)
+            if 0 <= j < QUARTERS:
+                copy_quarter(j)
             if i + 1 < H_TILES:
                 rotate_on_vector(i + 1)
             if i < H_TILES:
                 transpose_back(i)
-            if i + 1 < H_TILES:
-                multiply_by_b(i + 1, 1)
-            if i < H_TILES:
                 take_out(i)
             if H_TILES <= i < H_TILES + ROW_TILES:
                 mi = i - H_TILES
@@ -387,4 +397,3 @@ def tile_linearrecurrentunitcell_kernel(
 
         for mi in range(ROW_TILES):
             add_to_y(mi, range(EARLY_GROUPS, H_GROUPS))
-            nc.sync.dma_start(out=out_0[mi * P : (mi + 1) * P, :], in_=y_sum[:, mi, :])

@@ -71,6 +71,19 @@ def tile_linearrecurrentunitcell_kernel(
         sum_bank = ctx.enter_context(tc.psum_pool(name="sum_bank", bufs=3))
         ctx.enter_context(tc.manual_schedule())
 
+        warm = keep.tile([P, WIDE], BF16)
+        nc.vector.memset(warm[:], 0.0)
+        warm_col = keep.tile([P, 1], F32)
+        nc.vector.memset(warm_col[:], 0.0)
+        nc.scalar.activation(out=warm_col[:], in_=warm_col[:], func=ACT.Exp)
+
+        def keep_warm(count):
+            ps = bank.tile([P, WIDE], F32, tag="new_ps_re", name="warm_ps")
+            for index in range(count):
+                nc.tensor.matmul(out=ps[:], lhsT=warm[:, 0:P], rhs=warm[:], start=True, stop=True)
+
+        keep_warm(4)
+
         vec_rows = keep.tile([P, P], BF16)
         nc.vector.memset(vec_rows[:], 0.0)
         for v, vec in enumerate((nu, theta, gamma)):
@@ -79,8 +92,13 @@ def tile_linearrecurrentunitcell_kernel(
                 in_=vec.rearrange("(r j) -> r j", j=P),
             )
 
-        u_sb = keep.tile([P, ROW_TILES, N_IN], BF16)
-        nc.sync.dma_start(out=u_sb[:], in_=inputs.rearrange("(mi p) k -> p mi k", p=P))
+        u_sb = []
+        for kp in range(IN_PASSES):
+            u_sb.append(keep.tile([P, ROW_TILES, K_PASS], BF16, name="u_%d" % kp))
+            nc.sync.dma_start(
+                out=u_sb[kp][:],
+                in_=inputs.rearrange("(mi p) k -> p mi k", p=P)[:, :, kp * K_PASS : (kp + 1) * K_PASS],
+            )
 
         b_planes = keep.tile([P, H], U8, align_bytes=64)
         nc.vector.memset(b_planes[:].bitcast(I32), 0)
@@ -114,21 +132,24 @@ def tile_linearrecurrentunitcell_kernel(
                         .bitcast(I32),
                     )
 
-        for c in range(2):
-            for quad in range(4):
-                nc.sync.dma_start(
-                    out=c_planes[32 * quad : 32 * quad + 16, c, :].bitcast(I32),
-                    in_=c_scales_in[c][:, 4 * quad : 4 * quad + 4, :].bitcast(I32),
-                )
         c_words = keep.tile([P, 2, H_GROUPS, N_IN], U32, align_bytes=64)
-        for g in range(H_GROUPS):
+
+        def load_c_planes():
+            for c in range(2):
+                for quad in range(4):
+                    nc.sync.dma_start(
+                        out=c_planes[32 * quad : 32 * quad + 16, c, :].bitcast(I32),
+                        in_=c_scales_in[c][:, 4 * quad : 4 * quad + 4, :].bitcast(I32),
+                    )
+
+        def load_c(g):
             for c in range(2):
                 nc.sync.dma_start(
                     out=c_words[:, c, g, :].bitcast(I32),
                     in_=c_words_in[c][g].rearrange("p n t -> p (n t)").bitcast(I32),
                 )
+
         d_all = keep.tile([P, N_IN], BF16)
-        nc.sync.dma_start(out=d_all[:], in_=D.partition_broadcast(P))
 
         ident_bf16 = keep.tile([P, P], BF16)
         make_identity(nc, ident_bf16[:])
@@ -166,6 +187,8 @@ def tile_linearrecurrentunitcell_kernel(
         nc.scalar.activation(out=decay[:], in_=nu_cols, func=ACT.Exp)
         nc.scalar.activation(out=decay[:], in_=decay[:], func=ACT.Exp, scale=-1.0)
 
+        nc.scalar.activation(out=warm_col[:], in_=warm_col[:], func=ACT.Sin)
+
         angle = keep.tile([P, 2 * H_TILES], F32)
         nc.vector.tensor_copy(out=angle[:, 0:H_TILES], in_=theta_cols)
         nc.vector.tensor_scalar_add(out=angle[:, H_TILES : 2 * H_TILES], in0=theta_cols, scalar1=0.5 * math.pi)
@@ -186,6 +209,7 @@ def tile_linearrecurrentunitcell_kernel(
         sin_cos = keep.tile([P, 2 * H_TILES], F32)
         nc.scalar.activation(out=sin_cos[:], in_=angle[:], func=ACT.Sin)
 
+        keep_warm(3)
         u_words = keep.tile([P, IN_PASSES, ROWS], U32, align_bytes=64)
         u_planes = keep.tile([P, IN_PASSES, ROWS], U8, align_bytes=64)
         for kp in range(IN_PASSES):
@@ -194,21 +218,22 @@ def tile_linearrecurrentunitcell_kernel(
                 words_ps = sum_bank.tile([P, 2, 2 * P], F32, tag="mx_sum", name="u_words_ps")
                 transpose_words(
                     words_ps,
-                    lambda mi, half: u_sb[:, mi, :].bitcast(F32)[:, 2 * P * kp + half : 2 * P * (kp + 1) : 2],
+                    lambda mi, half: u_sb[kp][:, mi, :].bitcast(F32)[:, half::2],
                     rows_half,
                 )
-                copy = nc.scalar.copy if rows_half == 0 else nc.vector.tensor_copy
+                copy = nc.scalar.copy if kp == 1 and rows_half == 0 else nc.vector.tensor_copy
                 lay_side_by_side(copy, u_grouped, words_ps, rows_half)
             nc.vector.quantize_mx(
                 out=u_words[:, kp, :].bitcast(FP8X4), scales=u_planes[:, kp, :], in_=u_grouped[:]
             )
-
-        lam_re = keep.tile([P, H_TILES], F32)
-        nc.vector.tensor_mul(out=lam_re[:], in0=decay[:], in1=sin_cos[:, H_TILES : 2 * H_TILES])
-        lam_im = keep.tile([P, H_TILES], F32)
-        nc.vector.tensor_mul(out=lam_im[:], in0=decay[:], in1=sin_cos[:, 0:H_TILES])
-        neg_lam_im = keep.tile([P, H_TILES], F32)
-        nc.vector.tensor_scalar_mul(out=neg_lam_im[:], in0=lam_im[:], scalar1=-1.0)
+            keep_warm(1)
+            if kp == 0:
+                lam_re = keep.tile([P, H_TILES], F32)
+                nc.vector.tensor_mul(out=lam_re[:], in0=decay[:], in1=sin_cos[:, H_TILES : 2 * H_TILES])
+                lam_im = keep.tile([P, H_TILES], F32)
+                nc.vector.tensor_mul(out=lam_im[:], in0=decay[:], in1=sin_cos[:, 0:H_TILES])
+                neg_lam_im = keep.tile([P, H_TILES], F32)
+                nc.vector.tensor_scalar_mul(out=neg_lam_im[:], in0=lam_im[:], scalar1=-1.0)
 
         state_t = {}
         product = {}
@@ -223,8 +248,8 @@ def tile_linearrecurrentunitcell_kernel(
         x_planes = keep.tile([P, 2, H_GROUPS, ROWS], U8, align_bytes=64)
         y_sum = keep.tile([P, ROW_TILES, N_IN], F32)
 
-        def transpose_state(i, c):
-            t = bank.tile([P, ROWS], BF16, tag="state_t_%s" % PARTS[c], name="state_t_%s" % PARTS[c])
+        def transpose_state(i, c, home):
+            t = bank.tile([P, ROWS], BF16, tag=home, name="state_t_%s" % PARTS[c])
             for mi in range(ROW_TILES):
                 nc.tensor.matmul(
                     out=t[:, mi * P : (mi + 1) * P],
@@ -312,22 +337,22 @@ def tile_linearrecurrentunitcell_kernel(
                         in_=new_rows[(g, c)][:],
                     )
 
-        def transpose_quarter(j):
+        def transpose_quarter(j, home):
             g, rest = divmod(j, 4)
             c, rows_half = divmod(rest, 2)
-            word_tiles[j] = bank.tile([P, 2, 2 * P], F32, name="new_words_ps")
+            word_tiles[j] = bank.tile([P, 2, 2 * P], F32, tag=home, name="new_words_ps")
             transpose_words(
                 word_tiles[j],
                 lambda mi, half: new_bf16[(g, c)][:, mi, half].rearrange("p q e -> p (q e)").bitcast(F32),
                 rows_half,
             )
 
-        def copy_quarter(j):
+        def copy_quarter(j, copy):
             g, rest = divmod(j, 4)
             c, rows_half = divmod(rest, 2)
             if rows_half == 0:
                 new_grouped[(g, c)] = quant_pool.tile([P, 4 * ROWS], BF16, align_bytes=64, name="grouped")
-            lay_side_by_side(nc.scalar.copy, new_grouped[(g, c)], word_tiles[j], rows_half)
+            lay_side_by_side(copy, new_grouped[(g, c)], word_tiles[j], rows_half)
 
         def quantise_new(pair):
             g, c = divmod(pair, 2)
@@ -358,42 +383,82 @@ def tile_linearrecurrentunitcell_kernel(
         QUARTERS = 4 * H_GROUPS
         QUARTER_LAG = TILES_PER_GROUP + 1
         QUANTISE_LAG = QUARTER_LAG + 2
-        transpose_state(0, 0)
+        transpose_state(0, 0, "state_t_re")
         rotate_on_scalar(0)
-        transpose_state(0, 1)
+        transpose_state(0, 1, "state_t_im")
+        transpose_state(1, 0, "new_words")
         rotate_on_vector(0)
-        transpose_state(1, 0)
-        rotate_on_scalar(1)
         multiply_by_b(0, 0)
         multiply_by_b(0, 1)
-        for i in range(QUARTERS + QUANTISE_LAG - 1):
+        rotate_on_scalar(1)
+        for i in range(H_TILES - 1):
             j = i - QUARTER_LAG
+            if i == 5:
+                load_c_planes()
+            if i == 5:
+                load_c(0)
+            if i == 5:
+                load_c(1)
+            if i == 9:
+                load_c(2)
+            if i == 9:
+                load_c(3)
+            if i == 9:
+                nc.sync.dma_start(out=d_all[:], in_=D.partition_broadcast(P))
             if i + 1 < H_TILES:
-                transpose_state(i + 1, 1)
+                transpose_state(i + 1, 1, "state_t_im")
                 multiply_by_b(i + 1, 0)
             if i + 2 < H_TILES:
-                transpose_state(i + 2, 0)
+                transpose_state(i + 2, 0, "state_t_re")
             if i < H_TILES:
                 add_product(i)
             if i + 1 < H_TILES:
                 multiply_by_b(i + 1, 1)
             if 0 <= j < QUARTERS:
-                transpose_quarter(j)
+                transpose_quarter(j, "new_words")
             if i >= QUANTISE_LAG and (i - QUANTISE_LAG) % 2 == 0:
                 quantise_new((i - QUANTISE_LAG) // 2)
             if i + 2 < H_TILES:
                 rotate_on_scalar(i + 2)
             if 0 <= j < QUARTERS:
-                copy_quarter(j)
+                copy_quarter(j, nc.scalar.copy)
             if i + 1 < H_TILES:
                 rotate_on_vector(i + 1)
             if i < H_TILES:
                 transpose_back(i)
                 take_out(i)
-            if H_TILES <= i < H_TILES + ROW_TILES:
-                mi = i - H_TILES
-                nc.vector.tensor_mul(out=y_sum[:, mi, :], in0=u_sb[:, mi, :], in1=d_all[:])
-                add_to_y(mi, range(EARLY_GROUPS))
 
+        def scale_inputs(mi):
+            for kp in range(IN_PASSES):
+                cols = slice(kp * K_PASS, (kp + 1) * K_PASS)
+                nc.vector.tensor_mul(out=y_sum[:, mi, cols], in0=u_sb[kp][:, mi, :], in1=d_all[:, cols])
+
+        add_product(15)
+        transpose_quarter(10, "new_words")
+        quantise_new(4)
+        copy_quarter(10, nc.scalar.copy)
+        scale_inputs(0)
+        add_to_y(0, range(EARLY_GROUPS))
+        transpose_back(15)
+        take_out(15)
+        transpose_quarter(11, "state_t_re")
+        copy_quarter(11, nc.scalar.copy)
+        scale_inputs(1)
+        add_to_y(1, range(EARLY_GROUPS))
+        quantise_new(5)
+        scale_inputs(2)
+        scale_inputs(3)
+        transpose_quarter(12, "new_words")
+        transpose_quarter(13, "state_t_im")
+        copy_quarter(12, nc.scalar.copy)
+        copy_quarter(13, nc.scalar.copy)
+        quantise_new(6)
+        add_to_y(2, range(EARLY_GROUPS))
+        transpose_quarter(14, "state_t_re")
+        transpose_quarter(15, "new_words")
+        copy_quarter(14, nc.scalar.copy)
+        copy_quarter(15, nc.scalar.copy)
+        quantise_new(7)
+        add_to_y(3, range(EARLY_GROUPS))
         for mi in range(ROW_TILES):
             add_to_y(mi, range(EARLY_GROUPS, H_GROUPS))

@@ -65,7 +65,8 @@ def tile_linearrecurrentunitcell_kernel(
     with ExitStack() as ctx:
         keep = ctx.enter_context(tc.tile_pool(name="keep", bufs=1))
         acc_pool = ctx.enter_context(tc.tile_pool(name="acc", bufs=3))
-        group_pool = ctx.enter_context(tc.tile_pool(name="group", bufs=2))
+        rows_pool = ctx.enter_context(tc.tile_pool(name="rows", bufs=3))
+        bf16_pool = ctx.enter_context(tc.tile_pool(name="bf16", bufs=2))
         quant_pool = ctx.enter_context(tc.tile_pool(name="quant", bufs=3))
         bank = ctx.enter_context(tc.psum_pool(name="bank", bufs=1))
         sum_bank = ctx.enter_context(tc.psum_pool(name="sum_bank", bufs=3))
@@ -86,18 +87,18 @@ def tile_linearrecurrentunitcell_kernel(
 
         vec_rows = keep.tile([P, P], BF16)
         nc.vector.memset(vec_rows[:], 0.0)
-        for v, vec in enumerate((nu, theta, gamma)):
-            nc.sync.dma_start(
-                out=vec_rows[v * H_TILES : (v + 1) * H_TILES, :],
-                in_=vec.rearrange("(r j) -> r j", j=P),
-            )
-
         u_sb = []
         for kp in range(IN_PASSES):
             u_sb.append(keep.tile([P, ROW_TILES, K_PASS], BF16, name="u_%d" % kp))
             nc.sync.dma_start(
                 out=u_sb[kp][:],
                 in_=inputs.rearrange("(mi p) k -> p mi k", p=P)[:, :, kp * K_PASS : (kp + 1) * K_PASS],
+            )
+
+        for v, vec in enumerate((nu, theta, gamma)):
+            nc.sync.dma_start(
+                out=vec_rows[v * H_TILES : (v + 1) * H_TILES, :],
+                in_=vec.rearrange("(r j) -> r j", j=P),
             )
 
         b_planes = keep.tile([P, H], U8, align_bytes=64)
@@ -116,21 +117,29 @@ def tile_linearrecurrentunitcell_kernel(
         state_sb = [
             keep.tile([P, ROW_TILES, H], BF16, name="state_%s" % part) for part in PARTS
         ]
-        for g in range(H_GROUPS):
-            cols = slice(g * K_PASS, (g + 1) * K_PASS)
+        def load_state(begin, end):
             for c in range(2):
                 nc.sync.dma_start(
-                    out=state_sb[c][:, :, cols],
-                    in_=state_in[c].rearrange("(mi p) h -> p mi h", p=P)[:, :, cols],
+                    out=state_sb[c][:, :, begin:end],
+                    in_=state_in[c].rearrange("(mi p) h -> p mi h", p=P)[:, :, begin:end],
                 )
+
+        def load_b(begin, end):
             for c in range(2):
                 for kp in range(IN_PASSES):
                     nc.sync.dma_start(
-                        out=b_words[:, c, kp, cols].bitcast(I32),
-                        in_=b_words_in[c][kp]
-                        .rearrange("p n t -> p (n t)")[:, 4 * g * K_PASS : 4 * (g + 1) * K_PASS]
-                        .bitcast(I32),
+                        out=b_words[:, c, kp, begin:end].bitcast(I32),
+                        in_=b_words_in[c][kp].rearrange("p n t -> p (n t)")[:, 4 * begin : 4 * end].bitcast(I32),
                     )
+
+        load_state(0, K_PASS)
+        load_b(0, K_PASS // 2)
+        load_b(K_PASS // 2, K_PASS)
+        load_state(K_PASS, 2 * K_PASS)
+        load_b(K_PASS, 2 * K_PASS)
+        load_state(2 * K_PASS, H)
+        load_b(2 * K_PASS, 3 * K_PASS)
+        load_b(3 * K_PASS, H)
 
         c_words = keep.tile([P, 2, H_GROUPS, N_IN], U32, align_bytes=64)
 
@@ -246,7 +255,7 @@ def tile_linearrecurrentunitcell_kernel(
 
         x_words = keep.tile([P, 2, H_GROUPS, ROWS], U32, align_bytes=64)
         x_planes = keep.tile([P, 2, H_GROUPS, ROWS], U8, align_bytes=64)
-        y_sum = keep.tile([P, ROW_TILES, N_IN], F32)
+        y_sum = []
 
         def transpose_state(i, c, home):
             t = bank.tile([P, ROWS], BF16, tag=home, name="state_t_%s" % PARTS[c])
@@ -312,16 +321,16 @@ def tile_linearrecurrentunitcell_kernel(
                     nc.tensor.transpose(t[:, mi, :], new_t[(i, c)][:, mi * P : (mi + 1) * P], ident_f32[:])
                 new_ps[(i, c)] = t
 
-        def take_out(i):
+        def take_out(i, engine):
             g, a = divmod(i, TILES_PER_GROUP)
             cols = slice(a * P, (a + 1) * P)
             for c in range(2):
                 if a == 0:
-                    new_rows[(g, c)] = group_pool.tile([P, ROW_TILES, K_PASS], F32, name="new_rows_%s" % PARTS[c])
-                    new_bf16[(g, c)] = group_pool.tile([P, ROW_TILES, 2, P, 2], BF16, name="new_bf16_%s" % PARTS[c])
+                    new_rows[(g, c)] = rows_pool.tile([P, ROW_TILES, K_PASS], F32, tag="rows_%s" % PARTS[c], name="new_rows")
+                    new_bf16[(g, c)] = bf16_pool.tile([P, ROW_TILES, 2, P, 2], BF16, name="new_bf16_%s" % PARTS[c])
                 nc.scalar.copy(out=new_rows[(g, c)][:, :, cols], in_=new_ps[(i, c)][:])
                 for half in range(2):
-                    nc.gpsimd.tensor_scalar(
+                    engine.tensor_scalar(
                         out=new_bf16[(g, c)][:, :, half, a * (P // 4) : (a + 1) * (P // 4), :],
                         in0=new_rows[(g, c)][:, :, cols].rearrange(
                             "p mi (q half e) -> p mi half q e", half=2, e=2
@@ -363,9 +372,11 @@ def tile_linearrecurrentunitcell_kernel(
         def add_to_y(mi, groups):
             rows = slice(mi * P, (mi + 1) * P)
             passes = [(g, c) for g in groups for c in range(2)]
-            for n in range(N_IN // WIDE):
-                cols = slice(n * WIDE, (n + 1) * WIDE)
-                acc = sum_bank.tile([P, WIDE], F32, tag="mx_sum", name="y_ps")
+            late = H_GROUPS - 1 in groups
+            ends = [WIDE, WIDE + WIDE // 2, N_IN] if late and mi == ROW_TILES - 1 else [WIDE, N_IN]
+            for begin, end in zip([0] + ends, ends):
+                cols = slice(begin, end)
+                acc = sum_bank.tile([P, end - begin], F32, tag="mx_sum", name="y_ps")
                 for index, (g, c) in enumerate(passes):
                     nc.tensor.matmul_mx(
                         out=acc[:],
@@ -376,9 +387,10 @@ def tile_linearrecurrentunitcell_kernel(
                         start=(index == 0),
                         stop=(index == len(passes) - 1),
                     )
-                nc.vector.tensor_add(out=y_sum[:, mi, cols], in0=acc[:], in1=y_sum[:, mi, cols])
-                if H_GROUPS - 1 in groups:
-                    nc.sync.dma_start(out=out_0[rows, cols], in_=y_sum[:, mi, cols])
+                y_part = y_sum[mi // 2][:, mi % 2, cols]
+                nc.vector.tensor_add(out=y_part, in0=acc[:], in1=y_part)
+                if late:
+                    nc.sync.dma_start(out=out_0[rows, cols], in_=y_part)
 
         QUARTERS = 4 * H_GROUPS
         QUARTER_LAG = TILES_PER_GROUP + 1
@@ -393,17 +405,17 @@ def tile_linearrecurrentunitcell_kernel(
         rotate_on_scalar(1)
         for i in range(H_TILES - 1):
             j = i - QUARTER_LAG
-            if i == 5:
+            if i == 4:
                 load_c_planes()
-            if i == 5:
+            if i == 4:
                 load_c(0)
-            if i == 5:
+            if i == 6:
                 load_c(1)
-            if i == 9:
+            if i == 8:
                 load_c(2)
-            if i == 9:
+            if i == 10:
                 load_c(3)
-            if i == 9:
+            if i == 8:
                 nc.sync.dma_start(out=d_all[:], in_=D.partition_broadcast(P))
             if i + 1 < H_TILES:
                 transpose_state(i + 1, 1, "state_t_im")
@@ -426,27 +438,29 @@ def tile_linearrecurrentunitcell_kernel(
                 rotate_on_vector(i + 1)
             if i < H_TILES:
                 transpose_back(i)
-                take_out(i)
+                take_out(i, nc.gpsimd)
 
         def scale_inputs(mi):
             for kp in range(IN_PASSES):
                 cols = slice(kp * K_PASS, (kp + 1) * K_PASS)
-                nc.vector.tensor_mul(out=y_sum[:, mi, cols], in0=u_sb[kp][:, mi, :], in1=d_all[:, cols])
+                nc.vector.tensor_mul(out=y_sum[mi // 2][:, mi % 2, cols], in0=u_sb[kp][:, mi, :], in1=d_all[:, cols])
 
+        for part in PARTS:
+            y_sum.append(rows_pool.tile([P, 2, N_IN], F32, tag="rows_%s" % part, name="y_sum"))
         add_product(15)
         transpose_quarter(10, "new_words")
-        quantise_new(4)
         copy_quarter(10, nc.scalar.copy)
         scale_inputs(0)
+        scale_inputs(1)
+        quantise_new(4)
         add_to_y(0, range(EARLY_GROUPS))
+        scale_inputs(2)
         transpose_back(15)
-        take_out(15)
+        take_out(15, nc.vector)
         transpose_quarter(11, "state_t_re")
         copy_quarter(11, nc.scalar.copy)
-        scale_inputs(1)
-        add_to_y(1, range(EARLY_GROUPS))
         quantise_new(5)
-        scale_inputs(2)
+        add_to_y(1, range(EARLY_GROUPS))
         scale_inputs(3)
         transpose_quarter(12, "new_words")
         transpose_quarter(13, "state_t_im")

@@ -72,11 +72,12 @@ def tile_linearrecurrentunitcell_kernel(
         sum_bank = ctx.enter_context(tc.psum_pool(name="sum_bank", bufs=3))
         ctx.enter_context(tc.manual_schedule())
 
+        vec_rows = keep.tile([P, P], BF16)
+        nc.vector.memset(vec_rows[:], 0.0)
         warm = keep.tile([P, WIDE], BF16)
         nc.vector.memset(warm[:], 0.0)
         warm_col = keep.tile([P, 1], F32)
         nc.vector.memset(warm_col[:], 0.0)
-        nc.scalar.activation(out=warm_col[:], in_=warm_col[:], func=ACT.Exp)
 
         def keep_warm(count):
             ps = bank.tile([P, WIDE], F32, tag="new_ps_re", name="warm_ps")
@@ -85,34 +86,21 @@ def tile_linearrecurrentunitcell_kernel(
 
         keep_warm(4)
 
-        vec_rows = keep.tile([P, P], BF16)
-        nc.vector.memset(vec_rows[:], 0.0)
-        u_sb = []
-        for kp in range(IN_PASSES):
-            u_sb.append(keep.tile([P, ROW_TILES, K_PASS], BF16, name="u_%d" % kp))
-            nc.sync.dma_start(
-                out=u_sb[kp][:],
-                in_=inputs.rearrange("(mi p) k -> p mi k", p=P)[:, :, kp * K_PASS : (kp + 1) * K_PASS],
-            )
-
         for v, vec in enumerate((nu, theta, gamma)):
-            nc.sync.dma_start(
+            nc.scalar.dma_start(
                 out=vec_rows[v * H_TILES : (v + 1) * H_TILES, :],
                 in_=vec.rearrange("(r j) -> r j", j=P),
             )
+
+        nc.scalar.activation(out=warm_col[:], in_=warm_col[:], func=ACT.Exp)
+        u_sb = keep.tile([P, ROW_TILES, N_IN], BF16)
+        for mi in range(ROW_TILES):
+            nc.sync.dma_start(out=u_sb[:, mi, :], in_=inputs[mi * P : (mi + 1) * P, :])
 
         b_planes = keep.tile([P, H], U8, align_bytes=64)
         nc.vector.memset(b_planes[:].bitcast(I32), 0)
         c_planes = keep.tile([P, 2, N_IN], U8, align_bytes=64)
         nc.vector.memset(c_planes[:].bitcast(I32), 0)
-        for c in range(2):
-            for quad in range(4):
-                first = 32 * quad + 8 * c
-                nc.sync.dma_start(
-                    out=b_planes[first : first + 8, :].bitcast(I32),
-                    in_=b_scales_in[c][:, 4 * quad : 4 * quad + 4, :].bitcast(I32),
-                )
-
         b_words = keep.tile([P, 2, IN_PASSES, H], U32, align_bytes=64)
         state_sb = [
             keep.tile([P, ROW_TILES, H], BF16, name="state_%s" % part) for part in PARTS
@@ -132,8 +120,19 @@ def tile_linearrecurrentunitcell_kernel(
                         in_=b_words_in[c][kp].rearrange("p n t -> p (n t)")[:, 4 * begin : 4 * end].bitcast(I32),
                     )
 
-        load_state(0, K_PASS)
+        def load_b_planes():
+            for c in range(2):
+                for quad in range(4):
+                    first = 32 * quad + 8 * c
+                    nc.sync.dma_start(
+                        out=b_planes[first : first + 8, :].bitcast(I32),
+                        in_=b_scales_in[c][:, 4 * quad : 4 * quad + 4, :].bitcast(I32),
+                    )
+
+        load_state(0, K_PASS // 2)
+        load_b_planes()
         load_b(0, K_PASS // 2)
+        load_state(K_PASS // 2, K_PASS)
         load_b(K_PASS // 2, K_PASS)
         load_state(K_PASS, 2 * K_PASS)
         load_b(K_PASS, 2 * K_PASS)
@@ -218,31 +217,46 @@ def tile_linearrecurrentunitcell_kernel(
         sin_cos = keep.tile([P, 2 * H_TILES], F32)
         nc.scalar.activation(out=sin_cos[:], in_=angle[:], func=ACT.Sin)
 
-        keep_warm(3)
         u_words = keep.tile([P, IN_PASSES, ROWS], U32, align_bytes=64)
         u_planes = keep.tile([P, IN_PASSES, ROWS], U8, align_bytes=64)
-        for kp in range(IN_PASSES):
-            u_grouped = quant_pool.tile([P, 4 * ROWS], BF16, align_bytes=64, name="grouped")
-            for rows_half in range(2):
-                words_ps = sum_bank.tile([P, 2, 2 * P], F32, tag="mx_sum", name="u_words_ps")
+        u_grouped = [
+            quant_pool.tile([P, 4 * ROWS], BF16, align_bytes=64, tag="grouped", name="u_grouped") for kp in range(IN_PASSES)
+        ]
+        u_ps = {}
+        keep_warm(2)
+        for rows_half in range(2):
+            for kp in range(IN_PASSES):
+                if rows_half == 1 and kp == 1:
+                    words_ps = bank.tile([P, 2, 2 * P], F32, tag="new_ps_im", name="u_words_ps")
+                else:
+                    words_ps = sum_bank.tile([P, 2, 2 * P], F32, tag="mx_sum", name="u_words_ps")
                 transpose_words(
                     words_ps,
-                    lambda mi, half: u_sb[kp][:, mi, :].bitcast(F32)[:, half::2],
+                    lambda mi, half: u_sb[:, mi, kp * K_PASS : (kp + 1) * K_PASS].bitcast(F32)[:, half::2],
                     rows_half,
                 )
-                copy = nc.scalar.copy if kp == 1 and rows_half == 0 else nc.vector.tensor_copy
-                lay_side_by_side(copy, u_grouped, words_ps, rows_half)
+                u_ps[(kp, rows_half)] = words_ps
+        def quantise_u(kp, rows_half):
+            rows = slice(rows_half * 2 * P, (rows_half + 1) * 2 * P)
             nc.vector.quantize_mx(
-                out=u_words[:, kp, :].bitcast(FP8X4), scales=u_planes[:, kp, :], in_=u_grouped[:]
+                out=u_words[:, kp, rows].bitcast(FP8X4),
+                scales=u_planes[:, kp, rows],
+                in_=u_grouped[kp][:, rows_half * 8 * P : (rows_half + 1) * 8 * P],
             )
-            keep_warm(1)
-            if kp == 0:
-                lam_re = keep.tile([P, H_TILES], F32)
-                nc.vector.tensor_mul(out=lam_re[:], in0=decay[:], in1=sin_cos[:, H_TILES : 2 * H_TILES])
-                lam_im = keep.tile([P, H_TILES], F32)
-                nc.vector.tensor_mul(out=lam_im[:], in0=decay[:], in1=sin_cos[:, 0:H_TILES])
-                neg_lam_im = keep.tile([P, H_TILES], F32)
-                nc.vector.tensor_scalar_mul(out=neg_lam_im[:], in0=lam_im[:], scalar1=-1.0)
+        lay_side_by_side(nc.vector.tensor_copy, u_grouped[0], u_ps[(0, 0)], 0)
+        lay_side_by_side(nc.vector.tensor_copy, u_grouped[1], u_ps[(1, 0)], 0)
+        lay_side_by_side(nc.scalar.copy, u_grouped[0], u_ps[(0, 1)], 1)
+        quantise_u(0, 0)
+        lay_side_by_side(nc.vector.tensor_copy, u_grouped[1], u_ps[(1, 1)], 1)
+        quantise_u(1, 0)
+        quantise_u(0, 1)
+        quantise_u(1, 1)
+        lam_re = keep.tile([P, H_TILES], F32)
+        nc.vector.tensor_mul(out=lam_re[:], in0=decay[:], in1=sin_cos[:, H_TILES : 2 * H_TILES])
+        lam_im = keep.tile([P, H_TILES], F32)
+        nc.vector.tensor_mul(out=lam_im[:], in0=decay[:], in1=sin_cos[:, 0:H_TILES])
+        neg_lam_im = keep.tile([P, H_TILES], F32)
+        nc.vector.tensor_scalar_mul(out=neg_lam_im[:], in0=lam_im[:], scalar1=-1.0)
 
         state_t = {}
         product = {}
@@ -443,7 +457,7 @@ def tile_linearrecurrentunitcell_kernel(
         def scale_inputs(mi):
             for kp in range(IN_PASSES):
                 cols = slice(kp * K_PASS, (kp + 1) * K_PASS)
-                nc.vector.tensor_mul(out=y_sum[mi // 2][:, mi % 2, cols], in0=u_sb[kp][:, mi, :], in1=d_all[:, cols])
+                nc.vector.tensor_mul(out=y_sum[mi // 2][:, mi % 2, cols], in0=u_sb[:, mi, cols], in1=d_all[:, cols])
 
         for part in PARTS:
             y_sum.append(rows_pool.tile([P, 2, N_IN], F32, tag="rows_%s" % part, name="y_sum"))

@@ -67,6 +67,7 @@ def tile_linearrecurrentunitcell_kernel(
         acc_pool = ctx.enter_context(tc.tile_pool(name="acc", bufs=3))
         rows_pool = ctx.enter_context(tc.tile_pool(name="rows", bufs=3))
         bf16_pool = ctx.enter_context(tc.tile_pool(name="bf16", bufs=2))
+        b_pool = ctx.enter_context(tc.tile_pool(name="b_group", bufs=4))
         quant_pool = ctx.enter_context(tc.tile_pool(name="quant", bufs=3))
         bank = ctx.enter_context(tc.psum_pool(name="bank", bufs=1))
         sum_bank = ctx.enter_context(tc.psum_pool(name="sum_bank", bufs=3))
@@ -101,7 +102,10 @@ def tile_linearrecurrentunitcell_kernel(
         nc.vector.memset(b_planes[:].bitcast(I32), 0)
         c_planes = keep.tile([P, 2, N_IN], U8, align_bytes=64)
         nc.vector.memset(c_planes[:].bitcast(I32), 0)
-        b_words = keep.tile([P, 2, IN_PASSES, H], U32, align_bytes=64)
+        b_words = [
+            b_pool.tile([P, 2, IN_PASSES, K_PASS], U32, align_bytes=64, tag="group", name="b_words")
+            for g in range(H_GROUPS)
+        ]
         state_sb = [
             keep.tile([P, ROW_TILES, H], BF16, name="state_%s" % part) for part in PARTS
         ]
@@ -116,7 +120,7 @@ def tile_linearrecurrentunitcell_kernel(
             for c in range(2):
                 for kp in range(IN_PASSES):
                     nc.sync.dma_start(
-                        out=b_words[:, c, kp, begin:end].bitcast(I32),
+                        out=b_words[begin // K_PASS][:, c, kp, begin % K_PASS : begin % K_PASS + end - begin].bitcast(I32),
                         in_=b_words_in[c][kp].rearrange("p n t -> p (n t)")[:, 4 * begin : 4 * end].bitcast(I32),
                     )
 
@@ -308,7 +312,7 @@ def tile_linearrecurrentunitcell_kernel(
             for kp in range(IN_PASSES):
                 nc.tensor.matmul_mx(
                     out=acc[:],
-                    lhsT=b_words[:, c, kp, cols].bitcast(FP8X4),
+                    lhsT=b_words[i // TILES_PER_GROUP][:, c, kp, i % TILES_PER_GROUP * P : (i % TILES_PER_GROUP + 1) * P].bitcast(FP8X4),
                     lhsT_scale=b_planes[8 * c + 4 * kp : P, cols],
                     rhs=u_words[:, kp, :].bitcast(FP8X4),
                     rhs_scale=u_planes[:, kp, :],
@@ -421,15 +425,11 @@ def tile_linearrecurrentunitcell_kernel(
             j = i - QUARTER_LAG
             if i == 4:
                 load_c_planes()
-            if i == 4:
                 load_c(0)
-            if i == 6:
                 load_c(1)
-            if i == 8:
+            if i == 6:
                 load_c(2)
-            if i == 10:
                 load_c(3)
-            if i == 8:
                 nc.sync.dma_start(out=d_all[:], in_=D.partition_broadcast(P))
             if i + 1 < H_TILES:
                 transpose_state(i + 1, 1, "state_t_im")
@@ -459,8 +459,8 @@ def tile_linearrecurrentunitcell_kernel(
                 cols = slice(kp * K_PASS, (kp + 1) * K_PASS)
                 nc.vector.tensor_mul(out=y_sum[mi // 2][:, mi % 2, cols], in0=u_sb[:, mi, cols], in1=d_all[:, cols])
 
-        for part in PARTS:
-            y_sum.append(rows_pool.tile([P, 2, N_IN], F32, tag="rows_%s" % part, name="y_sum"))
+        for pair in range(2):
+            y_sum.append(b_pool.tile([P, 2, N_IN], F32, align_bytes=64, tag="group", name="y_sum"))
         add_product(15)
         transpose_quarter(10, "new_words")
         copy_quarter(10, nc.scalar.copy)

@@ -32,7 +32,6 @@ TWO_PI_HIGH = 6.28125
 TWO_PI_LOW = 2.0 * math.pi - TWO_PI_HIGH
 PI_INSIDE = 3.1415925
 
-
 def tile_linearrecurrentunitcell_kernel(
     tc,
     inputs,
@@ -95,8 +94,11 @@ def tile_linearrecurrentunitcell_kernel(
 
         nc.scalar.activation(out=warm_col[:], in_=warm_col[:], func=ACT.Exp)
         u_sb = keep.tile([P, ROW_TILES, N_IN], BF16)
-        for mi in range(ROW_TILES):
-            nc.sync.dma_start(out=u_sb[:, mi, :], in_=inputs[mi * P : (mi + 1) * P, :])
+        for rows_half in range(2):
+            nc.sync.dma_start(
+                out=u_sb[:, 2 * rows_half : 2 * rows_half + 2, :],
+                in_=inputs.rearrange("(mi p) k -> p mi k", p=P)[:, 2 * rows_half : 2 * rows_half + 2, :],
+            )
 
         b_planes = keep.tile([P, H], U8, align_bytes=64)
         nc.vector.memset(b_planes[:].bitcast(I32), 0)
@@ -250,17 +252,17 @@ def tile_linearrecurrentunitcell_kernel(
         lay_side_by_side(nc.vector.tensor_copy, u_grouped[0], u_ps[(0, 0)], 0)
         lay_side_by_side(nc.vector.tensor_copy, u_grouped[1], u_ps[(1, 0)], 0)
         lay_side_by_side(nc.scalar.copy, u_grouped[0], u_ps[(0, 1)], 1)
-        quantise_u(0, 0)
-        lay_side_by_side(nc.vector.tensor_copy, u_grouped[1], u_ps[(1, 1)], 1)
-        quantise_u(1, 0)
-        quantise_u(0, 1)
-        quantise_u(1, 1)
         lam_re = keep.tile([P, H_TILES], F32)
         nc.vector.tensor_mul(out=lam_re[:], in0=decay[:], in1=sin_cos[:, H_TILES : 2 * H_TILES])
         lam_im = keep.tile([P, H_TILES], F32)
         nc.vector.tensor_mul(out=lam_im[:], in0=decay[:], in1=sin_cos[:, 0:H_TILES])
         neg_lam_im = keep.tile([P, H_TILES], F32)
         nc.vector.tensor_scalar_mul(out=neg_lam_im[:], in0=lam_im[:], scalar1=-1.0)
+        quantise_u(0, 0)
+        lay_side_by_side(nc.vector.tensor_copy, u_grouped[1], u_ps[(1, 1)], 1)
+        quantise_u(1, 0)
+        quantise_u(0, 1)
+        quantise_u(1, 1)
 
         state_t = {}
         product = {}
@@ -418,6 +420,7 @@ def tile_linearrecurrentunitcell_kernel(
         transpose_state(0, 1, "state_t_im")
         transpose_state(1, 0, "new_words")
         rotate_on_vector(0)
+        keep_warm(3)
         multiply_by_b(0, 0)
         multiply_by_b(0, 1)
         rotate_on_scalar(1)

@@ -74,6 +74,16 @@ def tile_linearrecurrentunitcell_kernel(
 
         vec_rows = keep.tile([P, P], BF16)
         nc.vector.memset(vec_rows[:], 0.0)
+        u_sb = keep.tile([P, ROW_TILES, N_IN], BF16)
+        inputs_by_tile = inputs.rearrange("(mi p) k -> p mi k", p=P)
+        nc.sync.dma_start(out=u_sb[:, 0:2, :], in_=inputs_by_tile[:, 0:2, :])
+        for v, vec in enumerate((nu, theta, gamma)):
+            nc.sync.dma_start(
+                out=vec_rows[v * H_TILES : (v + 1) * H_TILES, :],
+                in_=vec.rearrange("(r j) -> r j", j=P),
+            )
+        nc.sync.dma_start(out=u_sb[:, 2:4, :], in_=inputs_by_tile[:, 2:4, :])
+
         warm = keep.tile([P, WIDE], BF16)
         nc.vector.memset(warm[:], 0.0)
         warm_col = keep.tile([P, 1], F32)
@@ -86,19 +96,8 @@ def tile_linearrecurrentunitcell_kernel(
 
         keep_warm(4)
 
-        for v, vec in enumerate((nu, theta, gamma)):
-            nc.scalar.dma_start(
-                out=vec_rows[v * H_TILES : (v + 1) * H_TILES, :],
-                in_=vec.rearrange("(r j) -> r j", j=P),
-            )
 
         nc.scalar.activation(out=warm_col[:], in_=warm_col[:], func=ACT.Exp)
-        u_sb = keep.tile([P, ROW_TILES, N_IN], BF16)
-        for rows_half in range(2):
-            nc.sync.dma_start(
-                out=u_sb[:, 2 * rows_half : 2 * rows_half + 2, :],
-                in_=inputs.rearrange("(mi p) k -> p mi k", p=P)[:, 2 * rows_half : 2 * rows_half + 2, :],
-            )
 
         b_planes = keep.tile([P, H], U8, align_bytes=64)
         nc.vector.memset(b_planes[:].bitcast(I32), 0)
@@ -420,7 +419,7 @@ def tile_linearrecurrentunitcell_kernel(
         transpose_state(0, 1, "state_t_im")
         transpose_state(1, 0, "new_words")
         rotate_on_vector(0)
-        keep_warm(3)
+        keep_warm(1)
         multiply_by_b(0, 0)
         multiply_by_b(0, 1)
         rotate_on_scalar(1)

@@ -190,37 +190,7 @@ def tile_linearrecurrentunitcell_kernel(
 
         vec_ps = bank.tile([P, P], BF16, tag="state_t_re", name="vec_ps")
         nc.tensor.transpose(vec_ps[:], vec_rows[:], ident_bf16[:])
-        vec_cols = keep.tile([P, 3 * H_TILES], F32)
-        nc.vector.tensor_copy(out=vec_cols[:], in_=vec_ps[:, 0 : 3 * H_TILES])
-        nu_cols = vec_cols[:, 0:H_TILES]
-        theta_cols = vec_cols[:, H_TILES : 2 * H_TILES]
-        gamma_cols = vec_cols[:, 2 * H_TILES : 3 * H_TILES]
-
-        decay = keep.tile([P, H_TILES], F32)
-        nc.scalar.activation(out=decay[:], in_=nu_cols, func=ACT.Exp)
-        nc.scalar.activation(out=decay[:], in_=decay[:], func=ACT.Exp, scale=-1.0)
-
-        nc.scalar.activation(out=warm_col[:], in_=warm_col[:], func=ACT.Sin)
-
-        angle = keep.tile([P, 2 * H_TILES], F32)
-        nc.vector.tensor_copy(out=angle[:, 0:H_TILES], in_=theta_cols)
-        nc.vector.tensor_scalar_add(out=angle[:, H_TILES : 2 * H_TILES], in0=theta_cols, scalar1=0.5 * math.pi)
-        turns = keep.tile([P, 2 * H_TILES], F32)
-        nc.vector.tensor_scalar(
-            out=turns[:], in0=angle[:], scalar1=0.5 / math.pi, scalar2=ROUND_MAGIC, op0=ALU.mult, op1=ALU.add
-        )
-        nc.vector.tensor_scalar_add(out=turns[:], in0=turns[:], scalar1=-ROUND_MAGIC)
-        nc.vector.scalar_tensor_tensor(
-            out=angle[:], in0=turns[:], scalar=-TWO_PI_HIGH, in1=angle[:], op0=ALU.mult, op1=ALU.add
-        )
-        nc.vector.scalar_tensor_tensor(
-            out=angle[:], in0=turns[:], scalar=-TWO_PI_LOW, in1=angle[:], op0=ALU.mult, op1=ALU.add
-        )
-        nc.vector.tensor_scalar(
-            out=angle[:], in0=angle[:], scalar1=PI_INSIDE, scalar2=-PI_INSIDE, op0=ALU.min, op1=ALU.max
-        )
-        sin_cos = keep.tile([P, 2 * H_TILES], F32)
-        nc.scalar.activation(out=sin_cos[:], in_=angle[:], func=ACT.Sin)
+        theta_ps = vec_ps[:, H_TILES : 2 * H_TILES]
 
         u_words = keep.tile([P, IN_PASSES, ROWS], U32, align_bytes=64)
         u_planes = keep.tile([P, IN_PASSES, ROWS], U8, align_bytes=64)
@@ -241,6 +211,10 @@ def tile_linearrecurrentunitcell_kernel(
                     rows_half,
                 )
                 u_ps[(kp, rows_half)] = words_ps
+
+        def copy_u(copy, kp, rows_half):
+            lay_side_by_side(copy, u_grouped[kp], u_ps[(kp, rows_half)], rows_half)
+
         def quantise_u(kp, rows_half):
             rows = slice(rows_half * 2 * P, (rows_half + 1) * 2 * P)
             nc.vector.quantize_mx(
@@ -248,18 +222,47 @@ def tile_linearrecurrentunitcell_kernel(
                 scales=u_planes[:, kp, rows],
                 in_=u_grouped[kp][:, rows_half * 8 * P : (rows_half + 1) * 8 * P],
             )
-        lay_side_by_side(nc.vector.tensor_copy, u_grouped[0], u_ps[(0, 0)], 0)
-        lay_side_by_side(nc.vector.tensor_copy, u_grouped[1], u_ps[(1, 0)], 0)
-        lay_side_by_side(nc.scalar.copy, u_grouped[0], u_ps[(0, 1)], 1)
+
+        decay = keep.tile([P, H_TILES], F32)
+        nc.scalar.activation(out=decay[:], in_=vec_ps[:, 0:H_TILES], func=ACT.Exp)
+        nc.scalar.activation(out=decay[:], in_=decay[:], func=ACT.Exp, scale=-1.0)
+        nc.scalar.activation(out=warm_col[:], in_=warm_col[:], func=ACT.Sin)
+
+        angle = keep.tile([P, 2 * H_TILES], F32)
+        turns = keep.tile([P, 2 * H_TILES], F32)
+        sin_cos = keep.tile([P, 2 * H_TILES], F32)
+        nc.vector.tensor_copy(out=angle[:, 0:H_TILES], in_=theta_ps)
+        nc.vector.tensor_scalar_add(out=angle[:, H_TILES : 2 * H_TILES], in0=theta_ps, scalar1=0.5 * math.pi)
+        gamma_cols = keep.tile([P, H_TILES], F32)
+        nc.vector.tensor_copy(out=gamma_cols[:], in_=vec_ps[:, 2 * H_TILES : 3 * H_TILES])
+        nc.vector.tensor_scalar(
+            out=turns[:], in0=angle[:], scalar1=0.5 / math.pi, scalar2=ROUND_MAGIC, op0=ALU.mult, op1=ALU.add
+        )
+        nc.vector.tensor_scalar_add(out=turns[:], in0=turns[:], scalar1=-ROUND_MAGIC)
+        copy_u(nc.vector.tensor_copy, 0, 0)
+        nc.vector.scalar_tensor_tensor(
+            out=angle[:], in0=turns[:], scalar=-TWO_PI_HIGH, in1=angle[:], op0=ALU.mult, op1=ALU.add
+        )
+        copy_u(nc.vector.tensor_copy, 1, 0)
+        nc.vector.scalar_tensor_tensor(
+            out=angle[:], in0=turns[:], scalar=-TWO_PI_LOW, in1=angle[:], op0=ALU.mult, op1=ALU.add
+        )
+        nc.vector.tensor_scalar(
+            out=angle[:], in0=angle[:], scalar1=PI_INSIDE, scalar2=-PI_INSIDE, op0=ALU.min, op1=ALU.max
+        )
+        nc.scalar.activation(out=sin_cos[:], in_=angle[:], func=ACT.Sin)
+        copy_u(nc.scalar.copy, 0, 1)
+        quantise_u(0, 0)
+        quantise_u(1, 0)
         lam_re = keep.tile([P, H_TILES], F32)
         nc.vector.tensor_mul(out=lam_re[:], in0=decay[:], in1=sin_cos[:, H_TILES : 2 * H_TILES])
         lam_im = keep.tile([P, H_TILES], F32)
         nc.vector.tensor_mul(out=lam_im[:], in0=decay[:], in1=sin_cos[:, 0:H_TILES])
         neg_lam_im = keep.tile([P, H_TILES], F32)
-        nc.vector.tensor_scalar_mul(out=neg_lam_im[:], in0=lam_im[:], scalar1=-1.0)
-        quantise_u(0, 0)
-        lay_side_by_side(nc.vector.tensor_copy, u_grouped[1], u_ps[(1, 1)], 1)
-        quantise_u(1, 0)
+        nc.vector.scalar_tensor_tensor(
+            out=neg_lam_im[:], in0=decay[:], scalar=-1.0, in1=sin_cos[:, 0:H_TILES], op0=ALU.mult, op1=ALU.mult
+        )
+        copy_u(nc.vector.tensor_copy, 1, 1)
         quantise_u(0, 1)
         quantise_u(1, 1)
 
@@ -435,9 +438,10 @@ def tile_linearrecurrentunitcell_kernel(
                 nc.sync.dma_start(out=d_all[:], in_=D.partition_broadcast(P))
             if i + 1 < H_TILES:
                 transpose_state(i + 1, 1, "state_t_im")
-                multiply_by_b(i + 1, 0)
             if i + 2 < H_TILES:
                 transpose_state(i + 2, 0, "state_t_re")
+            if i + 1 < H_TILES:
+                multiply_by_b(i + 1, 0)
             if i < H_TILES:
                 add_product(i)
             if i + 1 < H_TILES:

@@ -99,12 +99,12 @@ def tile_linearrecurrentunitcell_kernel(
 
         nc.scalar.activation(out=warm_col[:], in_=warm_col[:], func=ACT.Exp)
 
-        b_planes = keep.tile([P, H], U8, align_bytes=64)
+        b_planes = keep.tile([P, H], U8, align_bytes=256)
         nc.vector.memset(b_planes[:].bitcast(I32), 0)
-        c_planes = keep.tile([P, 2, N_IN], U8, align_bytes=64)
+        c_planes = keep.tile([P, 2, N_IN], U8, align_bytes=256)
         nc.vector.memset(c_planes[:].bitcast(I32), 0)
         b_words = [
-            b_pool.tile([P, 2, IN_PASSES, K_PASS], U32, align_bytes=64, tag="group", name="b_words")
+            b_pool.tile([P, 2, IN_PASSES, K_PASS], U32, align_bytes=256, tag="group", name="b_words")
             for g in range(H_GROUPS)
         ]
         state_sb = [
@@ -145,7 +145,7 @@ def tile_linearrecurrentunitcell_kernel(
         load_b(2 * K_PASS, 3 * K_PASS)
         load_b(3 * K_PASS, H)
 
-        c_words = keep.tile([P, 2, H_GROUPS, N_IN], U32, align_bytes=64)
+        c_words = keep.tile([P, 2, H_GROUPS, N_IN], U32, align_bytes=256)
 
         def load_c_planes():
             for c in range(2):
@@ -192,8 +192,8 @@ def tile_linearrecurrentunitcell_kernel(
         nc.tensor.transpose(vec_ps[:], vec_rows[:], ident_bf16[:])
         theta_ps = vec_ps[:, H_TILES : 2 * H_TILES]
 
-        u_words = keep.tile([P, IN_PASSES, ROWS], U32, align_bytes=64)
-        u_planes = keep.tile([P, IN_PASSES, ROWS], U8, align_bytes=64)
+        u_words = keep.tile([P, IN_PASSES, ROWS], U32, align_bytes=256)
+        u_planes = keep.tile([P, IN_PASSES, ROWS], U8, align_bytes=256)
         u_grouped = [
             quant_pool.tile([P, 4 * ROWS], BF16, align_bytes=64, tag="grouped", name="u_grouped") for kp in range(IN_PASSES)
         ]
@@ -275,8 +275,8 @@ def tile_linearrecurrentunitcell_kernel(
         new_grouped = {}
         word_tiles = {}
 
-        x_words = keep.tile([P, 2, H_GROUPS, ROWS], U32, align_bytes=64)
-        x_planes = keep.tile([P, 2, H_GROUPS, ROWS], U8, align_bytes=64)
+        x_words = keep.tile([P, 2, H_GROUPS, ROWS], U32, align_bytes=256)
+        x_planes = keep.tile([P, 2, H_GROUPS, ROWS], U8, align_bytes=256)
         y_sum = []
 
         def transpose_state(i, c, home):
@@ -466,7 +466,7 @@ def tile_linearrecurrentunitcell_kernel(
                 nc.vector.tensor_mul(out=y_sum[mi // 2][:, mi % 2, cols], in0=u_sb[:, mi, cols], in1=d_all[:, cols])
 
         for pair in range(2):
-            y_sum.append(b_pool.tile([P, 2, N_IN], F32, align_bytes=64, tag="group", name="y_sum"))
+            y_sum.append(b_pool.tile([P, 2, N_IN], F32, align_bytes=256, tag="group", name="y_sum"))
         add_product(15)
         transpose_quarter(10, "new_words")
         copy_quarter(10, nc.scalar.copy)

@@ -448,12 +448,16 @@ def tile_linearrecurrentunitcell_kernel(
                 multiply_by_b(i + 1, 1)
             if 0 <= j < QUARTERS:
                 transpose_quarter(j, "new_words")
+            if i == H_TILES - 2:
+                transpose_quarter(j + 1, "state_t_re")
             if i >= QUANTISE_LAG and (i - QUANTISE_LAG) % 2 == 0:
                 quantise_new((i - QUANTISE_LAG) // 2)
             if i + 2 < H_TILES:
                 rotate_on_scalar(i + 2)
             if 0 <= j < QUARTERS:
                 copy_quarter(j, nc.scalar.copy)
+            if i == H_TILES - 2:
+                copy_quarter(j + 1, nc.scalar.copy)
             if i + 1 < H_TILES:
                 rotate_on_vector(i + 1)
             if i < H_TILES:
@@ -468,8 +472,6 @@ def tile_linearrecurrentunitcell_kernel(
         for pair in range(2):
             y_sum.append(b_pool.tile([P, 2, N_IN], F32, align_bytes=256, tag="group", name="y_sum"))
         add_product(15)
-        transpose_quarter(10, "new_words")
-        copy_quarter(10, nc.scalar.copy)
         scale_inputs(0)
         scale_inputs(1)
         quantise_new(4)

import math
from contextlib import ExitStack

import concourse.mybir as mybir
from concourse.masks import make_identity

F32 = mybir.dt.float32
BF16 = mybir.dt.bfloat16
I32 = mybir.dt.int32
U32 = mybir.dt.uint32
U8 = mybir.dt.uint8
FP8X4 = mybir.dt.float8_e4m3fn_x4
ALU = mybir.AluOpType
ACT = mybir.ActivationFunctionType

P = 128
ROWS, N_IN, H = 512, 1024, 2048
K_PASS = 4 * P
WIDE = 512
ROW_TILES = ROWS // P
H_TILES = H // P
IN_PASSES = N_IN // K_PASS
H_GROUPS = H // K_PASS
TILES_PER_GROUP = K_PASS // P
EARLY_GROUPS = 2
PARTS = ("re", "im")

FLOPS = 2 * 2 * ROWS * N_IN * H + 2 * 2 * ROWS * H * N_IN

ROUND_MAGIC = 12582912.0
TWO_PI_HIGH = 6.28125
TWO_PI_LOW = 2.0 * math.pi - TWO_PI_HIGH
PI_INSIDE = 3.1415925

def tile_linearrecurrentunitcell_kernel(
    tc,
    inputs,
    state_re,
    state_im,
    B_re_words,
    B_re_scales,
    B_im_words,
    B_im_scales,
    C_re_words,
    C_re_scales,
    C_im_words,
    C_im_scales,
    D,
    nu,
    theta,
    gamma,
    out_0,
    out_1,
    out_2,
):
    nc = tc.nc
    state_in = (state_re, state_im)
    b_words_in = (B_re_words, B_im_words)
    b_scales_in = (B_re_scales, B_im_scales)
    c_words_in = (C_re_words, C_im_words)
    c_scales_in = (C_re_scales, C_im_scales)
    new_out = (out_1, out_2)

    with ExitStack() as ctx:
        keep = ctx.enter_context(tc.tile_pool(name="keep", bufs=1))
        acc_pool = ctx.enter_context(tc.tile_pool(name="acc", bufs=3))
        rows_pool = ctx.enter_context(tc.tile_pool(name="rows", bufs=3))
        bf16_pool = ctx.enter_context(tc.tile_pool(name="bf16", bufs=2))
        b_pool = ctx.enter_context(tc.tile_pool(name="b_group", bufs=4))
        quant_pool = ctx.enter_context(tc.tile_pool(name="quant", bufs=3))
        bank = ctx.enter_context(tc.psum_pool(name="bank", bufs=1))
        sum_bank = ctx.enter_context(tc.psum_pool(name="sum_bank", bufs=3))
        ctx.enter_context(tc.manual_schedule())

        vec_rows = keep.tile([P, P], BF16)
        nc.vector.memset(vec_rows[:], 0.0)
        u_sb = keep.tile([P, ROW_TILES, N_IN], BF16)
        inputs_by_tile = inputs.rearrange("(mi p) k -> p mi k", p=P)
        nc.sync.dma_start(out=u_sb[:, 0:2, :], in_=inputs_by_tile[:, 0:2, :])
        for v, vec in enumerate((nu, theta, gamma)):
            nc.sync.dma_start(
                out=vec_rows[v * H_TILES : (v + 1) * H_TILES, :],
                in_=vec.rearrange("(r j) -> r j", j=P),
            )
        nc.sync.dma_start(out=u_sb[:, 2:4, :], in_=inputs_by_tile[:, 2:4, :])

        warm = keep.tile([P, WIDE], BF16)
        nc.vector.memset(warm[:], 0.0)
        warm_col = keep.tile([P, 1], F32)
        nc.vector.memset(warm_col[:], 0.0)

        def keep_warm(count):
            ps = bank.tile([P, WIDE], F32, tag="new_ps_re", name="warm_ps")
            for index in range(count):
                nc.tensor.matmul(out=ps[:], lhsT=warm[:, 0:P], rhs=warm[:], start=True, stop=True)

        keep_warm(4)


        nc.scalar.activation(out=warm_col[:], in_=warm_col[:], func=ACT.Exp)

        b_planes = keep.tile([P, H], U8, align_bytes=256)
        nc.vector.memset(b_planes[:].bitcast(I32), 0)
        c_planes = keep.tile([P, 2, N_IN], U8, align_bytes=256)
        nc.vector.memset(c_planes[:].bitcast(I32), 0)
        b_words = [
            b_pool.tile([P, 2, IN_PASSES, K_PASS], U32, align_bytes=256, tag="group", name="b_words")
            for g in range(H_GROUPS)
        ]
        state_sb = [
            keep.tile([P, ROW_TILES, H], BF16, name="state_%s" % part) for part in PARTS
        ]
        def load_state(begin, end):
            for c in range(2):
                nc.sync.dma_start(
                    out=state_sb[c][:, :, begin:end],
                    in_=state_in[c].rearrange("(mi p) h -> p mi h", p=P)[:, :, begin:end],
                )

        def load_b(begin, end):
            for c in range(2):
                for kp in range(IN_PASSES):
                    nc.sync.dma_start(
                        out=b_words[begin // K_PASS][:, c, kp, begin % K_PASS : begin % K_PASS + end - begin].bitcast(I32),
                        in_=b_words_in[c][kp].rearrange("p n t -> p (n t)")[:, 4 * begin : 4 * end].bitcast(I32),
                    )

        def load_b_planes():
            for c in range(2):
                for quad in range(4):
                    first = 32 * quad + 8 * c
                    nc.sync.dma_start(
                        out=b_planes[first : first + 8, :].bitcast(I32),
                        in_=b_scales_in[c][:, 4 * quad : 4 * quad + 4, :].bitcast(I32),
                    )

        load_state(0, K_PASS // 2)
        load_b_planes()
        load_b(0, K_PASS // 2)
        load_state(K_PASS // 2, K_PASS)
        load_b(K_PASS // 2, K_PASS)
        load_state(K_PASS, 2 * K_PASS)
        load_b(K_PASS, 2 * K_PASS)
        load_state(2 * K_PASS, H)
        load_b(2 * K_PASS, 3 * K_PASS)
        load_b(3 * K_PASS, H)

        c_words = keep.tile([P, 2, H_GROUPS, N_IN], U32, align_bytes=256)

        def load_c_planes():
            for c in range(2):
                for quad in range(4):
                    nc.sync.dma_start(
                        out=c_planes[32 * quad : 32 * quad + 16, c, :].bitcast(I32),
                        in_=c_scales_in[c][:, 4 * quad : 4 * quad + 4, :].bitcast(I32),
                    )

        def load_c(g):
            for c in range(2):
                nc.sync.dma_start(
                    out=c_words[:, c, g, :].bitcast(I32),
                    in_=c_words_in[c][g].rearrange("p n t -> p (n t)").bitcast(I32),
                )

        d_all = keep.tile([P, N_IN], BF16)

        ident_bf16 = keep.tile([P, P], BF16)
        make_identity(nc, ident_bf16[:])
        ident_f32 = keep.tile([P, P], F32)
        make_identity(nc, ident_f32[:])

        def lay_side_by_side(engine_copy, grouped, words_ps, rows_half):
            engine_copy(
                out=grouped[:]
                .bitcast(F32)
                .rearrange("p (m half) -> p m half", half=2)[
                    :, rows_half * 2 * P : (rows_half + 1) * 2 * P, :
                ],
                in_=words_ps[:].rearrange("p half m -> p m half"),
            )

        def transpose_words(words_ps, words_of, rows_half):
            for half in range(2):
                for ml in range(2):
                    nc.tensor.transpose(
                        words_ps[:, half, ml * P : (ml + 1) * P],
                        words_of(2 * rows_half + ml, half),
                        ident_f32[:],
                    )

        vec_ps = bank.tile([P, P], BF16, tag="state_t_re", name="vec_ps")
        nc.tensor.transpose(vec_ps[:], vec_rows[:], ident_bf16[:])
        theta_ps = vec_ps[:, H_TILES : 2 * H_TILES]

        u_words = keep.tile([P, IN_PASSES, ROWS], U32, align_bytes=256)
        u_planes = keep.tile([P, IN_PASSES, ROWS], U8, align_bytes=256)
        u_grouped = [
            quant_pool.tile([P, 4 * ROWS], BF16, align_bytes=64, tag="grouped", name="u_grouped") for kp in range(IN_PASSES)
        ]
        u_ps = {}
        keep_warm(2)
        for rows_half in range(2):
            for kp in range(IN_PASSES):
                if rows_half == 1 and kp == 1:
                    words_ps = bank.tile([P, 2, 2 * P], F32, tag="new_ps_im", name="u_words_ps")
                else:
                    words_ps = sum_bank.tile([P, 2, 2 * P], F32, tag="mx_sum", name="u_words_ps")
                transpose_words(
                    words_ps,
                    lambda mi, half: u_sb[:, mi, kp * K_PASS : (kp + 1) * K_PASS].bitcast(F32)[:, half::2],
                    rows_half,
                )
                u_ps[(kp, rows_half)] = words_ps

        def copy_u(copy, kp, rows_half):
            lay_side_by_side(copy, u_grouped[kp], u_ps[(kp, rows_half)], rows_half)

        def quantise_u(kp, rows_half):
            rows = slice(rows_half * 2 * P, (rows_half + 1) * 2 * P)
            nc.vector.quantize_mx(
                out=u_words[:, kp, rows].bitcast(FP8X4),
                scales=u_planes[:, kp, rows],
                in_=u_grouped[kp][:, rows_half * 8 * P : (rows_half + 1) * 8 * P],
            )

        decay = keep.tile([P, H_TILES], F32)
        nc.scalar.activation(out=decay[:], in_=vec_ps[:, 0:H_TILES], func=ACT.Exp)
        nc.scalar.activation(out=decay[:], in_=decay[:], func=ACT.Exp, scale=-1.0)
        nc.scalar.activation(out=warm_col[:], in_=warm_col[:], func=ACT.Sin)

        angle = keep.tile([P, 2 * H_TILES], F32)
        turns = keep.tile([P, 2 * H_TILES], F32)
        sin_cos = keep.tile([P, 2 * H_TILES], F32)
        nc.vector.tensor_copy(out=angle[:, 0:H_TILES], in_=theta_ps)
        nc.vector.tensor_scalar_add(out=angle[:, H_TILES : 2 * H_TILES], in0=theta_ps, scalar1=0.5 * math.pi)
        gamma_cols = keep.tile([P, H_TILES], F32)
        nc.vector.tensor_copy(out=gamma_cols[:], in_=vec_ps[:, 2 * H_TILES : 3 * H_TILES])
        nc.vector.tensor_scalar(
            out=turns[:], in0=angle[:], scalar1=0.5 / math.pi, scalar2=ROUND_MAGIC, op0=ALU.mult, op1=ALU.add
        )
        nc.vector.tensor_scalar_add(out=turns[:], in0=turns[:], scalar1=-ROUND_MAGIC)
        copy_u(nc.vector.tensor_copy, 0, 0)
        nc.vector.scalar_tensor_tensor(
            out=angle[:], in0=turns[:], scalar=-TWO_PI_HIGH, in1=angle[:], op0=ALU.mult, op1=ALU.add
        )
        copy_u(nc.vector.tensor_copy, 1, 0)
        nc.vector.scalar_tensor_tensor(
            out=angle[:], in0=turns[:], scalar=-TWO_PI_LOW, in1=angle[:], op0=ALU.mult, op1=ALU.add
        )
        nc.vector.tensor_scalar(
            out=angle[:], in0=angle[:], scalar1=PI_INSIDE, scalar2=-PI_INSIDE, op0=ALU.min, op1=ALU.max
        )
        nc.scalar.activation(out=sin_cos[:], in_=angle[:], func=ACT.Sin)
        copy_u(nc.scalar.copy, 0, 1)
        quantise_u(0, 0)
        quantise_u(1, 0)
        lam_re = keep.tile([P, H_TILES], F32)
        nc.vector.tensor_mul(out=lam_re[:], in0=decay[:], in1=sin_cos[:, H_TILES : 2 * H_TILES])
        lam_im = keep.tile([P, H_TILES], F32)
        nc.vector.tensor_mul(out=lam_im[:], in0=decay[:], in1=sin_cos[:, 0:H_TILES])
        neg_lam_im = keep.tile([P, H_TILES], F32)
        nc.vector.scalar_tensor_tensor(
            out=neg_lam_im[:], in0=decay[:], scalar=-1.0, in1=sin_cos[:, 0:H_TILES], op0=ALU.mult, op1=ALU.mult
        )
        copy_u(nc.vector.tensor_copy, 1, 1)
        quantise_u(0, 1)
        quantise_u(1, 1)

        state_t = {}
        product = {}
        new_t = {}
        new_ps = {}
        new_rows = {}
        new_bf16 = {}
        new_grouped = {}
        word_tiles = {}

        x_words = keep.tile([P, 2, H_GROUPS, ROWS], U32, align_bytes=256)
        x_planes = keep.tile([P, 2, H_GROUPS, ROWS], U8, align_bytes=256)
        y_sum = []

        def transpose_state(i, c, home):
            t = bank.tile([P, ROWS], BF16, tag=home, name="state_t_%s" % PARTS[c])
            for mi in range(ROW_TILES):
                nc.tensor.matmul(
                    out=t[:, mi * P : (mi + 1) * P],
                    lhsT=state_sb[c][:, mi, i * P : (i + 1) * P],
                    rhs=ident_bf16[:],
                    start=True,
                    stop=True,
                )
            state_t[(i, c)] = t

        def rotate_on_scalar(i):
            one = slice(i, i + 1)
            for c, lam in enumerate((lam_re, lam_im)):
                t = acc_pool.tile([P, ROWS], F32, name="new_t_%s" % PARTS[c])
                nc.scalar.activation(out=t[:], in_=state_t[(i, 0)][:], func=ACT.Copy, scale=lam[:, one])
                new_t[(i, c)] = t

        def rotate_on_vector(i):
            one = slice(i, i + 1)
            for c, lam in enumerate((neg_lam_im, lam_re)):
                nc.vector.scalar_tensor_tensor(
                    out=new_t[(i, c)][:],
                    in0=state_t[(i, 1)][:],
                    scalar=lam[:, one],
                    in1=new_t[(i, c)][:],
                    op0=ALU.mult,
                    op1=ALU.add,
                )

        def multiply_by_b(i, c):
            cols = slice(i * P, (i + 1) * P)
            acc = sum_bank.tile([P, ROWS], F32, tag="mx_sum", name="product_%s" % PARTS[c])
            for kp in range(IN_PASSES):
                nc.tensor.matmul_mx(
                    out=acc[:],
                    lhsT=b_words[i // TILES_PER_GROUP][:, c, kp, i % TILES_PER_GROUP * P : (i % TILES_PER_GROUP + 1) * P].bitcast(FP8X4),
                    lhsT_scale=b_planes[8 * c + 4 * kp : P, cols],
                    rhs=u_words[:, kp, :].bitcast(FP8X4),
                    rhs_scale=u_planes[:, kp, :],
                    start=(kp == 0),
                    stop=(kp == IN_PASSES - 1),
                )
            product[(i, c)] = acc

        def add_product(i):
            for c in range(2):
                nc.vector.scalar_tensor_tensor(
                    out=new_t[(i, c)][:],
                    in0=product[(i, c)][:],
                    scalar=gamma_cols[:, i : i + 1],
                    in1=new_t[(i, c)][:],
                    op0=ALU.mult,
                    op1=ALU.add,
                )

        def transpose_back(i):
            for c in range(2):
                t = bank.tile([P, ROW_TILES, P], F32, tag="new_ps_%s" % PARTS[c], name="new_ps_%s" % PARTS[c])
                for mi in range(ROW_TILES):
                    nc.tensor.transpose(t[:, mi, :], new_t[(i, c)][:, mi * P : (mi + 1) * P], ident_f32[:])
                new_ps[(i, c)] = t

        def take_out(i, engine):
            g, a = divmod(i, TILES_PER_GROUP)
            cols = slice(a * P, (a + 1) * P)
            for c in range(2):
                if a == 0:
                    new_rows[(g, c)] = rows_pool.tile([P, ROW_TILES, K_PASS], F32, tag="rows_%s" % PARTS[c], name="new_rows")
                    new_bf16[(g, c)] = bf16_pool.tile([P, ROW_TILES, 2, P, 2], BF16, name="new_bf16_%s" % PARTS[c])
                nc.scalar.copy(out=new_rows[(g, c)][:, :, cols], in_=new_ps[(i, c)][:])
                for half in range(2):
                    engine.tensor_scalar(
                        out=new_bf16[(g, c)][:, :, half, a * (P // 4) : (a + 1) * (P // 4), :],
                        in0=new_rows[(g, c)][:, :, cols].rearrange(
                            "p mi (q half e) -> p mi half q e", half=2, e=2
                        )[:, :, half],
                        scalar1=(1.0 if c == 0 else -1.0),
                        scalar2=0.0,
                        op0=ALU.mult,
                        op1=ALU.add,
                    )
                if a == TILES_PER_GROUP - 1:
                    nc.sync.dma_start(
                        out=new_out[c].rearrange("(mi p) h -> p mi h", p=P)[:, :, g * K_PASS : (g + 1) * K_PASS],
                        in_=new_rows[(g, c)][:],
                    )

        def transpose_quarter(j, home):
            g, rest = divmod(j, 4)
            c, rows_half = divmod(rest, 2)
            word_tiles[j] = bank.tile([P, 2, 2 * P], F32, tag=home, name="new_words_ps")
            transpose_words(
                word_tiles[j],
                lambda mi, half: new_bf16[(g, c)][:, mi, half].rearrange("p q e -> p (q e)").bitcast(F32),
                rows_half,
            )

        def copy_quarter(j, copy):
            g, rest = divmod(j, 4)
            c, rows_half = divmod(rest, 2)
            if rows_half == 0:
                new_grouped[(g, c)] = quant_pool.tile([P, 4 * ROWS], BF16, align_bytes=64, name="grouped")
            lay_side_by_side(copy, new_grouped[(g, c)], word_tiles[j], rows_half)

        def quantise_new(pair):
            g, c = divmod(pair, 2)
            nc.vector.quantize_mx(
                out=x_words[:, c, g, :].bitcast(FP8X4), scales=x_planes[:, c, g, :], in_=new_grouped[(g, c)][:]
            )

        def add_to_y(mi, groups):
            rows = slice(mi * P, (mi + 1) * P)
            passes = [(g, c) for g in groups for c in range(2)]
            late = H_GROUPS - 1 in groups
            ends = [WIDE, WIDE + WIDE // 2, N_IN] if late and mi == ROW_TILES - 1 else [WIDE, N_IN]
            for begin, end in zip([0] + ends, ends):
                cols = slice(begin, end)
                acc = sum_bank.tile([P, end - begin], F32, tag="mx_sum", name="y_ps")
                for index, (g, c) in enumerate(passes):
                    nc.tensor.matmul_mx(
                        out=acc[:],
                        lhsT=x_words[:, c, g, rows].bitcast(FP8X4),
                        lhsT_scale=x_planes[:, c, g, rows],
                        rhs=c_words[:, c, g, cols].bitcast(FP8X4),
                        rhs_scale=c_planes[4 * g : P, c, cols],
                        start=(index == 0),
                        stop=(index == len(passes) - 1),
                    )
                y_part = y_sum[mi // 2][:, mi % 2, cols]
                nc.vector.tensor_add(out=y_part, in0=acc[:], in1=y_part)
                if late:
                    nc.sync.dma_start(out=out_0[rows, cols], in_=y_part)

        QUARTERS = 4 * H_GROUPS
        QUARTER_LAG = TILES_PER_GROUP + 1
        QUANTISE_LAG = QUARTER_LAG + 2
        transpose_state(0, 0, "state_t_re")
        rotate_on_scalar(0)
        transpose_state(0, 1, "state_t_im")
        transpose_state(1, 0, "new_words")
        rotate_on_vector(0)
        keep_warm(1)
        multiply_by_b(0, 0)
        multiply_by_b(0, 1)
        rotate_on_scalar(1)
        for i in range(H_TILES - 1):
            j = i - QUARTER_LAG
            if i == 4:
                load_c_planes()
                load_c(0)
                load_c(1)
            if i == 6:
                load_c(2)
                load_c(3)
                nc.sync.dma_start(out=d_all[:], in_=D.partition_broadcast(P))
            if i + 1 < H_TILES:
                transpose_state(i + 1, 1, "state_t_im")
            if i + 2 < H_TILES:
                transpose_state(i + 2, 0, "state_t_re")
            if i + 1 < H_TILES:
                multiply_by_b(i + 1, 0)
            if i < H_TILES:
                add_product(i)
            if i + 1 < H_TILES:
                multiply_by_b(i + 1, 1)
            if 0 <= j < QUARTERS:
                transpose_quarter(j, "new_words")
            if i == H_TILES - 2:
                transpose_quarter(j + 1, "state_t_re")
            if i >= QUANTISE_LAG and (i - QUANTISE_LAG) % 2 == 0:
                quantise_new((i - QUANTISE_LAG) // 2)
            if i + 2 < H_TILES:
                rotate_on_scalar(i + 2)
            if 0 <= j < QUARTERS:
                copy_quarter(j, nc.scalar.copy)
            if i == H_TILES - 2:
                copy_quarter(j + 1, nc.scalar.copy)
            if i + 1 < H_TILES:
                rotate_on_vector(i + 1)
            if i < H_TILES:
                transpose_back(i)
                take_out(i, nc.gpsimd)

        def scale_inputs(mi):
            for kp in range(IN_PASSES):
                cols = slice(kp * K_PASS, (kp + 1) * K_PASS)
                nc.vector.tensor_mul(out=y_sum[mi // 2][:, mi % 2, cols], in0=u_sb[:, mi, cols], in1=d_all[:, cols])

        for pair in range(2):
            y_sum.append(b_pool.tile([P, 2, N_IN], F32, align_bytes=256, tag="group", name="y_sum"))
        add_product(15)
        scale_inputs(0)
        scale_inputs(1)
        quantise_new(4)
        add_to_y(0, range(EARLY_GROUPS))
        scale_inputs(2)
        transpose_back(15)
        take_out(15, nc.vector)
        transpose_quarter(11, "state_t_re")
        copy_quarter(11, nc.scalar.copy)
        quantise_new(5)
        add_to_y(1, range(EARLY_GROUPS))
        scale_inputs(3)
        transpose_quarter(12, "new_words")
        transpose_quarter(13, "state_t_im")
        copy_quarter(12, nc.scalar.copy)
        copy_quarter(13, nc.scalar.copy)
        quantise_new(6)
        add_to_y(2, range(EARLY_GROUPS))
        transpose_quarter(14, "state_t_re")
        transpose_quarter(15, "new_words")
        copy_quarter(14, nc.scalar.copy)
        copy_quarter(15, nc.scalar.copy)
        quantise_new(7)
        add_to_y(3, range(EARLY_GROUPS))
        for mi in range(ROW_TILES):
            add_to_y(mi, range(EARLY_GROUPS, H_GROUPS))
